import numpy as np
import ml_dtypes


def mxq(x, axis, fmt="e4m3"):
    dtype, down = {"e4m3": (ml_dtypes.float8_e4m3fn, 7), "e5m2": (ml_dtypes.float8_e5m2, 14)}[fmt]
    v = np.moveaxis(np.asarray(x, np.float32).astype(ml_dtypes.bfloat16).astype(np.float64), axis, -1)
    blocks = v.reshape(v.shape[:-1] + (-1, 32))
    amax = np.abs(blocks).max(-1, keepdims=True)
    byte = np.maximum(np.where(amax > 0, np.frexp(amax)[1] - 1 + 127, 0) - down, 1)
    scale = np.exp2(byte - 127.0)
    codes = (blocks / scale).astype(np.float32).astype(dtype).astype(np.float64)
    return np.moveaxis((codes * scale).reshape(v.shape), -1, axis)


WIDE = False


def mx_kscale(k):
    if not WIDE:
        return np.ones(k)
    levels = np.array([10, -10, 5, -5, 0])
    a = np.random.permutation(np.resize(levels, k // 512 * 4)).reshape(k // 512, 4)
    idx = np.arange(k)
    return np.exp2(a[idx // 512, idx % 128 // 32])


BF16 = ml_dtypes.bfloat16


def bf(x):
    return np.asarray(x, np.float32).astype(BF16)


def f64(x):
    return np.asarray(x).astype(np.float64)


E2M1 = np.array([0.0, 0.5, 1.0, 1.5, 2.0, 3.0, 4.0, 6.0, -0.0, -0.5, -1.0, -1.5, -2.0, -3.0, -4.0, -6.0])


def pack_weight(w, fmt):
    k, n = w.shape
    w = f64(bf(w)).reshape(k // 32, 32, n)
    amax = np.abs(w).max(1)
    if fmt == "e4m3":
        byte = np.frexp(amax)[1] - 1 + 127 - 7
    else:
        mant, ex = np.frexp(amax / 6.0)
        byte = np.where(mant > 0.5, ex, ex - 1) + 127
    byte = np.clip(np.where(amax > 0, byte, 1), 1, 254)
    scaled = (w * np.exp2(127.0 - byte)[:, None, :]).reshape(k, n).astype(np.float32)
    by_word = np.ascontiguousarray(scaled.reshape(k // 512, 128, 4, n).transpose(0, 1, 3, 2))
    if fmt == "e4m3":
        words = by_word.astype(ml_dtypes.float8_e4m3fn).view(np.uint8)
    else:
        c = by_word.astype(ml_dtypes.float4_e2m1fn).view(np.uint8) & 0xF
        words = c[..., 0::2] | (c[..., 1::2] << 4)
    return np.ascontiguousarray(words), np.ascontiguousarray(byte.astype(np.uint8).reshape(k // 512, 16, n))


def unpack_weight(words, scales, fmt):
    g, p, n, _ = words.shape
    if fmt == "e4m3":
        vals = np.ascontiguousarray(words).view(ml_dtypes.float8_e4m3fn).astype(np.float64)
    else:
        nib = np.empty((g, p, n, 4), np.uint8)
        nib[..., 0::2] = words & 0xF
        nib[..., 1::2] = words >> 4
        vals = E2M1[nib]
    vals = vals * np.repeat(np.exp2(scales.astype(np.float64) - 127.0), 8, axis=1)[..., None]
    return vals.transpose(0, 1, 3, 2).reshape(g * 512, n)


B, E, D = 4096, 512, 256


def setup_inputs():
    s = mx_kscale(E)
    ws = 1.0 / np.sqrt(E)
    inputs = {
        "x": bf(np.random.standard_normal((B, E)) * s),
        "state_A": bf(np.random.uniform(0.0, 1.0, (B, D))),
        "state_B": bf(0.5 + np.random.uniform(0.0, 1.0, (B, D))),
        "state_p": bf(np.random.standard_normal((B, D))),
        "state_x": bf(np.random.standard_normal((B, E)) * s),
        "time_decay": bf(0.5 * np.random.standard_normal(D)),
        "time_first": bf(np.log(0.3) + 0.3 * np.random.standard_normal(D)),
        "time_mix_k": bf(np.random.uniform(0.0, 1.0, (1, E))),
        "time_mix_v": bf(np.random.uniform(0.0, 1.0, (1, E))),
    }
    w_key = np.random.standard_normal((D, E)) * ws / s[None, :]
    w_value = np.random.standard_normal((D, E)) * ws / s[None, :]
    inputs["W_key_words"], inputs["W_key_scales"] = pack_weight(np.ascontiguousarray(w_key.T), "e4m3")
    inputs["W_value_words"], inputs["W_value_scales"] = pack_weight(np.ascontiguousarray(w_value.T), "e4m3")
    return inputs


def reference(x, state_A, state_B, state_p, state_x, time_decay, time_first, time_mix_k, time_mix_v, W_key_words, W_key_scales, W_value_words, W_value_scales):
    x, state_x = f64(x), f64(state_x)
    state_A, state_B, state_p = f64(state_A), f64(state_B), f64(state_p)
    mk, mv = f64(time_mix_k), f64(time_mix_v)
    xk = x * mk + state_x * (1.0 - mk)
    xv = x * mv + state_x * (1.0 - mv)
    k = mxq(xk, 1, "e4m3") @ unpack_weight(W_key_words, W_key_scales, "e4m3")
    v = mxq(xv, 1, "e4m3") @ unpack_weight(W_value_words, W_value_scales, "e4m3")
    ww = f64(time_first) + k
    p = np.maximum(state_p, ww)
    e1 = np.exp(state_p - p)
    e2 = np.exp(ww - p)
    a = e1 * state_A + e2 * v
    b = e1 * state_B + e2
    td = -np.exp(f64(time_decay))
    ww = state_p + td
    p = np.maximum(ww, k)
    e1 = np.exp(ww - p)
    e2 = np.exp(k - p)
    new_A = e1 * state_A + e2 * v
    new_B = e1 * state_B + e2
    return (a, b, new_A, new_B, p)

@@ -1,0 +1,282 @@
+from contextlib import ExitStack
+
+import concourse.mybir as mybir
+from concourse.masks import make_identity
+
+BF16 = mybir.dt.bfloat16
+F32 = mybir.dt.float32
+I32 = mybir.dt.int32
+U8 = mybir.dt.uint8
+U32 = mybir.dt.uint32
+FP8X4 = mybir.dt.float8_e4m3fn_x4
+ALU = mybir.AluOpType
+FUNC = mybir.ActivationFunctionType
+
+P = 128
+PACK = 4
+ROWS, E, D = 4096, 512, 256
+TILES = ROWS // P
+GROUP = 4
+PAIR = 2
+GROUPS = TILES // GROUP
+GROUP_ROWS = GROUP * P
+QUADRANT = 32
+
+FLOPS = 2 * 2 * ROWS * E * D
+
+
+def tile_rwkv_timemix_for_quant_pa_t_kernel(
+    tc,
+    x,
+    state_A,
+    state_B,
+    state_p,
+    state_x,
+    time_decay,
+    time_first,
+    time_mix_k,
+    time_mix_v,
+    W_key_words,
+    W_key_scales,
+    W_value_words,
+    W_value_scales,
+    out_0,
+    out_1,
+    out_2,
+    out_3,
+    out_4,
+):
+    nc = tc.nc
+    by_tile = "(p t) c -> p t c"
+    x_rows = x.rearrange(by_tile, t=TILES)
+    sx_rows = state_x.rearrange(by_tile, t=TILES)
+    sp_rows = state_p.rearrange(by_tile, t=TILES)
+    sa_rows = state_A.rearrange(by_tile, t=TILES)
+    sb_rows = state_B.rearrange(by_tile, t=TILES)
+    a_rows = out_0.rearrange(by_tile, t=TILES)
+    b_rows = out_1.rearrange(by_tile, t=TILES)
+    new_a_rows = out_2.rearrange(by_tile, t=TILES)
+    new_b_rows = out_3.rearrange(by_tile, t=TILES)
+    new_p_rows = out_4.rearrange(by_tile, t=TILES)
+
+    with ExitStack() as pools:
+        const = pools.enter_context(tc.tile_pool(name="const", bufs=1))
+        loads = pools.enter_context(tc.tile_pool(name="loads", bufs=3))
+        mixing = pools.enter_context(tc.tile_pool(name="mixing", bufs=2))
+        work = pools.enter_context(tc.tile_pool(name="work", bufs=2))
+        results = pools.enter_context(tc.tile_pool(name="results", bufs=3))
+        psum_t = pools.enter_context(tc.psum_pool(name="psum_t", bufs=1))
+        psum_kv = pools.enter_context(tc.psum_pool(name="psum_kv", bufs=2))
+
+        def load_group(g):
+            tiles = slice(g * GROUP, (g + 1) * GROUP)
+            x_sb = loads.tile([P, GROUP, E], BF16, name="x_sb")
+            nc.sync.dma_start(out=x_sb[:], in_=x_rows[:, tiles, :])
+            sx_sb = loads.tile([P, GROUP, E], BF16, name="sx_sb")
+            nc.sync.dma_start(out=sx_sb[:], in_=sx_rows[:, tiles, :])
+            sp_sb = loads.tile([P, GROUP, D], BF16, name="sp_sb")
+            nc.sync.dma_start(out=sp_sb[:], in_=sp_rows[:, tiles, :])
+            sa_sb = loads.tile([P, GROUP, D], BF16, name="sa_sb")
+            nc.sync.dma_start(out=sa_sb[:], in_=sa_rows[:, tiles, :])
+            sb_sb = loads.tile([P, GROUP, D], BF16, name="sb_sb")
+            nc.sync.dma_start(out=sb_sb[:], in_=sb_rows[:, tiles, :])
+            return {"x": x_sb, "sx": sx_sb, "sp": sp_sb, "sa": sa_sb, "sb": sb_sb}
+
+        ident = const.tile([P, P], BF16, name="ident")
+        make_identity(nc, ident[:])
+
+        def load_mix(time_mix, label):
+            raw = const.tile([P, PACK], BF16, name="mix_raw_" + label)
+            nc.sync.dma_start(out=raw[:], in_=time_mix.rearrange("o (p j) -> (o p) j", j=PACK))
+            mix = const.tile([P, PACK], F32, name="mix_" + label)
+            nc.vector.tensor_copy(out=mix[:], in_=raw[:])
+            rest = const.tile([P, PACK], F32, name="rest_" + label)
+            nc.vector.tensor_scalar(
+                out=rest[:], in0=raw[:], scalar1=-1.0, scalar2=1.0, op0=ALU.mult, op1=ALU.add
+            )
+            return mix, rest
+
+        def load_weight(words, scales, label):
+            codes = const.tile([P, D * PACK], U8, name="w_codes_" + label, align_bytes=64)
+            nc.sync.dma_start(
+                out=codes[:].bitcast(I32),
+                in_=words[0].rearrange("p n t -> p (n t)").bitcast(I32),
+            )
+            plane = const.tile([P, D], U8, name="w_plane_" + label, align_bytes=64)
+            nc.vector.memset(plane[:].bitcast(I32), 0)
+            for q in range(P // QUADRANT):
+                nc.sync.dma_start(
+                    out=plane[q * QUADRANT : q * QUADRANT + PACK, :].bitcast(I32),
+                    in_=scales[0, q * PACK : (q + 1) * PACK, :].bitcast(I32),
+                )
+            return codes, plane
+
+        mix_k, rest_k = load_mix(time_mix_k, "k")
+        mix_v, rest_v = load_mix(time_mix_v, "v")
+        loaded = {0: load_group(0)}
+        wk_codes, wk_plane = load_weight(W_key_words, W_key_scales, "k")
+        wv_codes, wv_plane = load_weight(W_value_words, W_value_scales, "v")
+
+        tf_bf = const.tile([P, D], BF16, name="tf_bf")
+        nc.sync.dma_start(out=tf_bf[:], in_=time_first.partition_broadcast(P))
+        td_bf = const.tile([P, D], BF16, name="td_bf")
+        nc.sync.dma_start(out=td_bf[:], in_=time_decay.partition_broadcast(P))
+        decay = const.tile([P, D], F32, name="decay")
+        nc.scalar.activation(out=decay[:], in_=td_bf[:], func=FUNC.Exp)
+        shift = const.tile([P, 2, D], F32, name="shift")
+        nc.vector.tensor_scalar_mul(out=shift[:, 0, :], in0=tf_bf[:], scalar1=-1.0)
+        nc.vector.tensor_scalar_mul(out=shift[:, 1, :], in0=decay[:], scalar1=-1.0)
+
+        def transpose_group(rows_sb, label):
+            banks = []
+            for half in range(PACK // 2):
+                bank = psum_t.tile([P, 2, GROUP_ROWS], BF16, name="%s_t%d" % (label, half))
+                for jj in range(2):
+                    for i in range(GROUP):
+                        nc.tensor.transpose(
+                            out=bank[:, jj, i * P : (i + 1) * P],
+                            in_=rows_sb[:, i, 2 * half + jj : E : PACK],
+                            identity=ident[:],
+                        )
+                banks.append(bank)
+            return [banks[j // 2][:, j % 2, :] for j in range(PACK)]
+
+        def mix_and_quantise(group):
+            x_planes = transpose_group(group["x"], "x")
+            sx_planes = transpose_group(group["sx"], "sx")
+            streams = [("k", mix_k, rest_k), ("v", mix_v, rest_v)]
+            prev_part = {}
+            mixed = {}
+            for label, mix, rest in streams:
+                prev_part[label] = mixing.tile([P, PACK, GROUP_ROWS], F32, name="prev_part_" + label)
+                mixed[label] = mixing.tile([P, PACK, GROUP_ROWS], BF16, name="mixed_" + label)
+            for j in range(PACK):
+                for label, mix, rest in streams:
+                    nc.scalar.activation(
+                        out=prev_part[label][:, j, :],
+                        in_=sx_planes[j],
+                        func=FUNC.Copy,
+                        scale=rest[:, j : j + 1],
+                    )
+            for j in range(PACK):
+                for label, mix, rest in streams:
+                    nc.vector.scalar_tensor_tensor(
+                        out=mixed[label][:, j, :],
+                        in0=x_planes[j],
+                        scalar=mix[:, j : j + 1],
+                        in1=prev_part[label][:, j, :],
+                        op0=ALU.mult,
+                        op1=ALU.add,
+                    )
+            packed = {}
+            for label, mix, rest in streams:
+                grouped = mixing.tile(
+                    [P, GROUP_ROWS, PACK], BF16, name="grouped_" + label, align_bytes=64
+                )
+                nc.scalar.copy(
+                    out=grouped[:].rearrange("p (c i) j -> p c j i", i=4),
+                    in_=mixed[label][:].rearrange("p j (c i) -> p c j i", i=4),
+                )
+                codes = mixing.tile([P, GROUP_ROWS], U32, name="codes_" + label, align_bytes=64)
+                plane = mixing.tile([P, GROUP_ROWS], U8, name="plane_" + label, align_bytes=64)
+                nc.vector.quantize_mx(
+                    out=codes[:].bitcast(FP8X4),
+                    scales=plane[:],
+                    in_=grouped[:].rearrange("p r j -> p (r j)"),
+                )
+                packed[label] = (codes, plane)
+            return packed
+
+        def project(operand, w_codes, w_plane, first_tile, label):
+            codes, plane = operand
+            acc = psum_kv.tile([P, PAIR, D], F32, name="acc_" + label)
+            for i in range(PAIR):
+                cols = slice((first_tile + i) * P, (first_tile + i + 1) * P)
+                nc.tensor.matmul_mx(
+                    out=acc[:, i, :],
+                    lhsT=codes[:, cols].bitcast(FP8X4),
+                    lhsT_scale=plane[:, cols],
+                    rhs=w_codes[:].bitcast(FP8X4),
+                    rhs_scale=w_plane[:],
+                    start=True,
+                    stop=True,
+                )
+            return acc
+
+        def recurrence(g, h, group, packed):
+            first_tile = h * PAIR
+            tiles = slice(first_tile, first_tile + PAIR)
+            out_tiles = slice(g * GROUP + first_tile, g * GROUP + first_tile + PAIR)
+            k_ps = project(packed["k"], wk_codes, wk_plane, first_tile, "k")
+            v_ps = project(packed["v"], wv_codes, wv_plane, first_tile, "v")
+
+            both = [P, 2, PAIR, D]
+            flat = [P, 2, PAIR * D]
+
+            def twice(ap):
+                return ap.rearrange("p i d -> p (i d)").unsqueeze(1).to_broadcast(flat)
+
+            def flat_view(tile_ap):
+                return tile_ap.rearrange("p w i d -> p w (i d)")
+
+            gap = work.tile([P, PAIR, D], F32, name="gap")
+            nc.vector.tensor_tensor(out=gap[:], in0=group["sp"][:, tiles, :], in1=k_ps[:], op=ALU.subtract)
+            lead = work.tile(both, F32, name="lead")
+            nc.vector.tensor_tensor(
+                out=lead[:],
+                in0=gap[:].unsqueeze(1).to_broadcast(both),
+                in1=shift[:].unsqueeze(2).to_broadcast(both),
+                op=ALU.add,
+            )
+            new_p = results.tile([P, PAIR, D], F32, name="new_p")
+            nc.vector.scalar_tensor_tensor(
+                out=new_p[:].rearrange("p i d -> p (i d)"),
+                in0=lead[:, 1, :, :].rearrange("p i d -> p (i d)"),
+                scalar=0.0,
+                in1=k_ps[:].rearrange("p i d -> p (i d)"),
+                op0=ALU.max,
+                op1=ALU.add,
+            )
+            nc.sync.dma_start(out=new_p_rows[:, out_tiles, :], in_=new_p[:])
+            old_w = work.tile(both, F32, name="old_w")
+            nc.scalar.activation(out=old_w[:], in_=lead[:], func=FUNC.Exp)
+            new_w = work.tile(both, F32, name="new_w")
+            nc.scalar.activation(out=new_w[:], in_=lead[:], func=FUNC.Exp, scale=-1.0)
+
+            old_a = work.tile(both, F32, name="old_a")
+            nc.vector.scalar_tensor_tensor(
+                out=flat_view(old_a[:]), in0=flat_view(old_w[:]), scalar=1.0,
+                in1=twice(group["sa"][:, tiles, :]), op0=ALU.min, op1=ALU.mult,
+            )
+            old_b = work.tile(both, F32, name="old_b")
+            nc.vector.scalar_tensor_tensor(
+                out=flat_view(old_b[:]), in0=flat_view(old_w[:]), scalar=1.0,
+                in1=twice(group["sb"][:, tiles, :]), op0=ALU.min, op1=ALU.mult,
+            )
+            new_a = work.tile(both, F32, name="new_a")
+            nc.vector.scalar_tensor_tensor(
+                out=flat_view(new_a[:]), in0=flat_view(new_w[:]), scalar=1.0,
+                in1=twice(v_ps[:]), op0=ALU.min, op1=ALU.mult,
+            )
+            sum_b = results.tile(both, F32, name="sum_b")
+            nc.vector.scalar_tensor_tensor(
+                out=flat_view(sum_b[:]), in0=flat_view(new_w[:]), scalar=1.0,
+                in1=flat_view(old_b[:]), op0=ALU.min, op1=ALU.add,
+            )
+            sum_a = results.tile(both, F32, name="sum_a")
+            nc.vector.tensor_tensor(out=sum_a[:], in0=old_a[:], in1=new_a[:], op=ALU.add)
+
+            nc.sync.dma_start(out=b_rows[:, out_tiles, :], in_=sum_b[:, 0, :, :])
+            nc.sync.dma_start(out=new_b_rows[:, out_tiles, :], in_=sum_b[:, 1, :, :])
+            nc.sync.dma_start(out=a_rows[:, out_tiles, :], in_=sum_a[:, 0, :, :])
+            nc.sync.dma_start(out=new_a_rows[:, out_tiles, :], in_=sum_a[:, 1, :, :])
+
+        loaded[1] = load_group(1)
+        packed = {0: mix_and_quantise(loaded[0])}
+        for g in range(GROUPS):
+            if g + 2 < GROUPS:
+                loaded[g + 2] = load_group(g + 2)
+            if g + 1 < GROUPS:
+                packed[g + 1] = mix_and_quantise(loaded[g + 1])
+            for h in range(GROUP // PAIR):
+                recurrence(g, h, loaded[g], packed[g])

@@ -187,6 +187,19 @@ def tile_rwkv_timemix_for_quant_pa_t_kernel(
                 packed[label] = (codes, plane)
             return packed
 
+        def old_exponents(group):
+            old_exp = work.tile([P, 2, GROUP, D], F32, name="old_exp")
+            for w in range(2):
+                for h in range(GROUP // PAIR):
+                    tiles = slice(h * PAIR, (h + 1) * PAIR)
+                    nc.gpsimd.tensor_tensor(
+                        out=old_exp[:, w, tiles, :],
+                        in0=group["sp"][:, tiles, :],
+                        in1=shift[:, w, :].unsqueeze(1).to_broadcast([P, PAIR, D]),
+                        op=ALU.add,
+                    )
+            return old_exp
+
         def project(operand, w_codes, w_plane, first_tile, label):
             codes, plane = operand
             acc = psum_kv.tile([P, PAIR, D], F32, name="acc_" + label)
@@ -203,7 +216,7 @@ def tile_rwkv_timemix_for_quant_pa_t_kernel(
                 )
             return acc
 
-        def recurrence(g, h, group, packed):
+        def recurrence(g, h, group, packed, old_exp):
             first_tile = h * PAIR
             tiles = slice(first_tile, first_tile + PAIR)
             out_tiles = slice(g * GROUP + first_tile, g * GROUP + first_tile + PAIR)
@@ -219,24 +232,15 @@ def tile_rwkv_timemix_for_quant_pa_t_kernel(
             def flat_view(tile_ap):
                 return tile_ap.rearrange("p w i d -> p w (i d)")
 
-            gap = work.tile([P, PAIR, D], F32, name="gap")
-            nc.vector.tensor_tensor(out=gap[:], in0=group["sp"][:, tiles, :], in1=k_ps[:], op=ALU.subtract)
             lead = work.tile(both, F32, name="lead")
             nc.vector.tensor_tensor(
                 out=lead[:],
-                in0=gap[:].unsqueeze(1).to_broadcast(both),
-                in1=shift[:].unsqueeze(2).to_broadcast(both),
-                op=ALU.add,
+                in0=old_exp[:, :, tiles, :],
+                in1=k_ps[:].unsqueeze(1).to_broadcast(both),
+                op=ALU.subtract,
             )
             new_p = results.tile([P, PAIR, D], F32, name="new_p")
-            nc.vector.scalar_tensor_tensor(
-                out=new_p[:].rearrange("p i d -> p (i d)"),
-                in0=lead[:, 1, :, :].rearrange("p i d -> p (i d)"),
-                scalar=0.0,
-                in1=k_ps[:].rearrange("p i d -> p (i d)"),
-                op0=ALU.max,
-                op1=ALU.add,
-            )
+            nc.vector.tensor_tensor(out=new_p[:], in0=old_exp[:, 1, tiles, :], in1=k_ps[:], op=ALU.max)
             nc.sync.dma_start(out=new_p_rows[:, out_tiles, :], in_=new_p[:])
             old_w = work.tile(both, F32, name="old_w")
             nc.scalar.activation(out=old_w[:], in_=lead[:], func=FUNC.Exp)
@@ -264,7 +268,10 @@ def tile_rwkv_timemix_for_quant_pa_t_kernel(
                 in1=flat_view(old_b[:]), op0=ALU.min, op1=ALU.add,
             )
             sum_a = results.tile(both, F32, name="sum_a")
-            nc.vector.tensor_tensor(out=sum_a[:], in0=old_a[:], in1=new_a[:], op=ALU.add)
+            for w in range(2):
+                nc.gpsimd.tensor_tensor(
+                    out=sum_a[:, w, :, :], in0=old_a[:, w, :, :], in1=new_a[:, w, :, :], op=ALU.add
+                )
 
             nc.sync.dma_start(out=b_rows[:, out_tiles, :], in_=sum_b[:, 0, :, :])
             nc.sync.dma_start(out=new_b_rows[:, out_tiles, :], in_=sum_b[:, 1, :, :])
@@ -273,10 +280,12 @@ def tile_rwkv_timemix_for_quant_pa_t_kernel(
 
         loaded[1] = load_group(1)
         packed = {0: mix_and_quantise(loaded[0])}
+        old_exps = {0: old_exponents(loaded[0])}
         for g in range(GROUPS):
             if g + 2 < GROUPS:
                 loaded[g + 2] = load_group(g + 2)
             if g + 1 < GROUPS:
                 packed[g + 1] = mix_and_quantise(loaded[g + 1])
+                old_exps[g + 1] = old_exponents(loaded[g + 1])
             for h in range(GROUP // PAIR):
-                recurrence(g, h, loaded[g], packed[g])
+                recurrence(g, h, loaded[g], packed[g], old_exps[g])

@@ -62,18 +62,19 @@ def tile_rwkv_timemix_for_quant_pa_t_kernel(
     with ExitStack() as pools:
         const = pools.enter_context(tc.tile_pool(name="const", bufs=1))
         loads = pools.enter_context(tc.tile_pool(name="loads", bufs=3))
-        mixing = pools.enter_context(tc.tile_pool(name="mixing", bufs=2))
-        work = pools.enter_context(tc.tile_pool(name="work", bufs=2))
+        stage = pools.enter_context(tc.tile_pool(name="stage", bufs=1))
+        operands = pools.enter_context(tc.tile_pool(name="operands", bufs=2))
+        work = pools.enter_context(tc.tile_pool(name="work", bufs=3))
         results = pools.enter_context(tc.tile_pool(name="results", bufs=3))
         psum_t = pools.enter_context(tc.psum_pool(name="psum_t", bufs=1))
         psum_kv = pools.enter_context(tc.psum_pool(name="psum_kv", bufs=2))
 
         def load_group(g):
             tiles = slice(g * GROUP, (g + 1) * GROUP)
-            x_sb = loads.tile([P, GROUP, E], BF16, name="x_sb")
-            nc.sync.dma_start(out=x_sb[:], in_=x_rows[:, tiles, :])
             sx_sb = loads.tile([P, GROUP, E], BF16, name="sx_sb")
             nc.sync.dma_start(out=sx_sb[:], in_=sx_rows[:, tiles, :])
+            x_sb = loads.tile([P, GROUP, E], BF16, name="x_sb")
+            nc.sync.dma_start(out=x_sb[:], in_=x_rows[:, tiles, :])
             sp_sb = loads.tile([P, GROUP, D], BF16, name="sp_sb")
             nc.sync.dma_start(out=sp_sb[:], in_=sp_rows[:, tiles, :])
             sa_sb = loads.tile([P, GROUP, D], BF16, name="sa_sb")
@@ -127,39 +128,39 @@ def tile_rwkv_timemix_for_quant_pa_t_kernel(
         nc.vector.tensor_scalar_mul(out=shift[:, 0, :], in0=tf_bf[:], scalar1=-1.0)
         nc.vector.tensor_scalar_mul(out=shift[:, 1, :], in0=decay[:], scalar1=-1.0)
 
-        def transpose_group(rows_sb, label):
-            banks = []
-            for half in range(PACK // 2):
-                bank = psum_t.tile([P, 2, GROUP_ROWS], BF16, name="%s_t%d" % (label, half))
-                for jj in range(2):
-                    for i in range(GROUP):
-                        nc.tensor.transpose(
-                            out=bank[:, jj, i * P : (i + 1) * P],
-                            in_=rows_sb[:, i, 2 * half + jj : E : PACK],
-                            identity=ident[:],
-                        )
-                banks.append(bank)
-            return [banks[j // 2][:, j % 2, :] for j in range(PACK)]
+        def transpose_two_planes(rows_sb, first_plane, label):
+            bank = psum_t.tile([P, 2, GROUP_ROWS], BF16, name="%s_t%d" % (label, first_plane))
+            for jj in range(2):
+                for i in range(GROUP):
+                    nc.tensor.transpose(
+                        out=bank[:, jj, i * P : (i + 1) * P],
+                        in_=rows_sb[:, i, first_plane + jj : E : PACK],
+                        identity=ident[:],
+                    )
+            return [bank[:, jj, :] for jj in range(2)]
 
         def mix_and_quantise(group):
-            x_planes = transpose_group(group["x"], "x")
-            sx_planes = transpose_group(group["sx"], "sx")
+            x_planes = []
+            sx_planes = []
+            for first_plane in range(0, PACK, 2):
+                sx_planes.extend(transpose_two_planes(group["sx"], first_plane, "sx"))
+                x_planes.extend(transpose_two_planes(group["x"], first_plane, "x"))
             streams = [("k", mix_k, rest_k), ("v", mix_v, rest_v)]
             prev_part = {}
             mixed = {}
             for label, mix, rest in streams:
-                prev_part[label] = mixing.tile([P, PACK, GROUP_ROWS], F32, name="prev_part_" + label)
-                mixed[label] = mixing.tile([P, PACK, GROUP_ROWS], BF16, name="mixed_" + label)
-            for j in range(PACK):
-                for label, mix, rest in streams:
+                prev_part[label] = stage.tile([P, PACK, GROUP_ROWS], F32, name="prev_part_" + label)
+                mixed[label] = stage.tile([P, PACK, GROUP_ROWS], BF16, name="mixed_" + label)
+            for label, mix, rest in streams:
+                for j in range(PACK):
                     nc.scalar.activation(
                         out=prev_part[label][:, j, :],
                         in_=sx_planes[j],
                         func=FUNC.Copy,
                         scale=rest[:, j : j + 1],
                     )
-            for j in range(PACK):
-                for label, mix, rest in streams:
+            for label, mix, rest in streams:
+                for j in range(PACK):
                     nc.vector.scalar_tensor_tensor(
                         out=mixed[label][:, j, :],
                         in0=x_planes[j],
@@ -170,15 +171,15 @@ def tile_rwkv_timemix_for_quant_pa_t_kernel(
                     )
             packed = {}
             for label, mix, rest in streams:
-                grouped = mixing.tile(
+                grouped = stage.tile(
                     [P, GROUP_ROWS, PACK], BF16, name="grouped_" + label, align_bytes=64
                 )
                 nc.scalar.copy(
                     out=grouped[:].rearrange("p (c i) j -> p c j i", i=4),
                     in_=mixed[label][:].rearrange("p j (c i) -> p c j i", i=4),
                 )
-                codes = mixing.tile([P, GROUP_ROWS], U32, name="codes_" + label, align_bytes=64)
-                plane = mixing.tile([P, GROUP_ROWS], U8, name="plane_" + label, align_bytes=64)
+                codes = operands.tile([P, GROUP_ROWS], U32, name="codes_" + label, align_bytes=64)
+                plane = operands.tile([P, GROUP_ROWS], U8, name="plane_" + label, align_bytes=64)
                 nc.vector.quantize_mx(
                     out=codes[:].bitcast(FP8X4),
                     scales=plane[:],
@@ -186,19 +187,6 @@ def tile_rwkv_timemix_for_quant_pa_t_kernel(
                 )
                 packed[label] = (codes, plane)
             return packed
-
-        def old_exponents(group):
-            old_exp = work.tile([P, 2, GROUP, D], F32, name="old_exp")
-            for w in range(2):
-                for h in range(GROUP // PAIR):
-                    tiles = slice(h * PAIR, (h + 1) * PAIR)
-                    nc.gpsimd.tensor_tensor(
-                        out=old_exp[:, w, tiles, :],
-                        in0=group["sp"][:, tiles, :],
-                        in1=shift[:, w, :].unsqueeze(1).to_broadcast([P, PAIR, D]),
-                        op=ALU.add,
-                    )
-            return old_exp
 
         def project(operand, w_codes, w_plane, first_tile, label):
             codes, plane = operand
@@ -216,7 +204,7 @@ def tile_rwkv_timemix_for_quant_pa_t_kernel(
                 )
             return acc
 
-        def recurrence(g, h, group, packed, old_exp):
+        def recurrence(g, h, group, packed):
             first_tile = h * PAIR
             tiles = slice(first_tile, first_tile + PAIR)
             out_tiles = slice(g * GROUP + first_tile, g * GROUP + first_tile + PAIR)
@@ -232,42 +220,52 @@ def tile_rwkv_timemix_for_quant_pa_t_kernel(
             def flat_view(tile_ap):
                 return tile_ap.rearrange("p w i d -> p w (i d)")
 
+            gap = work.tile([P, PAIR, D], F32, name="gap")
+            nc.vector.tensor_tensor(out=gap[:], in0=group["sp"][:, tiles, :], in1=k_ps[:], op=ALU.subtract)
             lead = work.tile(both, F32, name="lead")
             nc.vector.tensor_tensor(
                 out=lead[:],
-                in0=old_exp[:, :, tiles, :],
-                in1=k_ps[:].unsqueeze(1).to_broadcast(both),
-                op=ALU.subtract,
+                in0=gap[:].unsqueeze(1).to_broadcast(both),
+                in1=shift[:].unsqueeze(2).to_broadcast(both),
+                op=ALU.add,
             )
             new_p = results.tile([P, PAIR, D], F32, name="new_p")
-            nc.vector.tensor_tensor(out=new_p[:], in0=old_exp[:, 1, tiles, :], in1=k_ps[:], op=ALU.max)
+            nc.vector.scalar_tensor_tensor(
+                out=new_p[:].rearrange("p i d -> p (i d)"),
+                in0=lead[:, 1, :, :].rearrange("p i d -> p (i d)"),
+                scalar=0.0,
+                in1=k_ps[:].rearrange("p i d -> p (i d)"),
+                op0=ALU.max,
+                op1=ALU.add,
+            )
             nc.sync.dma_start(out=new_p_rows[:, out_tiles, :], in_=new_p[:])
             old_w = work.tile(both, F32, name="old_w")
             nc.scalar.activation(out=old_w[:], in_=lead[:], func=FUNC.Exp)
+            excess = work.tile(both, F32, name="excess")
+            nc.scalar.activation(out=excess[:], in_=lead[:], func=FUNC.Relu)
             new_w = work.tile(both, F32, name="new_w")
-            nc.scalar.activation(out=new_w[:], in_=lead[:], func=FUNC.Exp, scale=-1.0)
+            nc.scalar.activation(out=new_w[:], in_=excess[:], func=FUNC.Exp, scale=-1.0)
 
-            old_a = work.tile(both, F32, name="old_a")
-            nc.vector.scalar_tensor_tensor(
-                out=flat_view(old_a[:]), in0=flat_view(old_w[:]), scalar=1.0,
-                in1=twice(group["sa"][:, tiles, :]), op0=ALU.min, op1=ALU.mult,
-            )
             old_b = work.tile(both, F32, name="old_b")
             nc.vector.scalar_tensor_tensor(
                 out=flat_view(old_b[:]), in0=flat_view(old_w[:]), scalar=1.0,
                 in1=twice(group["sb"][:, tiles, :]), op0=ALU.min, op1=ALU.mult,
             )
-            new_a = work.tile(both, F32, name="new_a")
+            old_a = work.tile(both, F32, name="old_a")
             nc.vector.scalar_tensor_tensor(
-                out=flat_view(new_a[:]), in0=flat_view(new_w[:]), scalar=1.0,
-                in1=twice(v_ps[:]), op0=ALU.min, op1=ALU.mult,
+                out=flat_view(old_a[:]), in0=flat_view(old_w[:]), scalar=1.0,
+                in1=twice(group["sa"][:, tiles, :]), op0=ALU.min, op1=ALU.mult,
+            )
+            new_a = work.tile(both, F32, name="new_a")
+            nc.vector.tensor_tensor(
+                out=flat_view(new_a[:]), in0=flat_view(new_w[:]), in1=twice(v_ps[:]), op=ALU.mult
             )
             sum_b = results.tile(both, F32, name="sum_b")
-            nc.vector.scalar_tensor_tensor(
-                out=flat_view(sum_b[:]), in0=flat_view(new_w[:]), scalar=1.0,
-                in1=flat_view(old_b[:]), op0=ALU.min, op1=ALU.add,
-            )
             sum_a = results.tile(both, F32, name="sum_a")
+            for w in range(2):
+                nc.gpsimd.tensor_tensor(
+                    out=sum_b[:, w, :, :], in0=old_b[:, w, :, :], in1=new_w[:, w, :, :], op=ALU.add
+                )
             for w in range(2):
                 nc.gpsimd.tensor_tensor(
                     out=sum_a[:, w, :, :], in0=old_a[:, w, :, :], in1=new_a[:, w, :, :], op=ALU.add
@@ -280,12 +278,10 @@ def tile_rwkv_timemix_for_quant_pa_t_kernel(
 
         loaded[1] = load_group(1)
         packed = {0: mix_and_quantise(loaded[0])}
-        old_exps = {0: old_exponents(loaded[0])}
         for g in range(GROUPS):
             if g + 2 < GROUPS:
                 loaded[g + 2] = load_group(g + 2)
             if g + 1 < GROUPS:
                 packed[g + 1] = mix_and_quantise(loaded[g + 1])
-                old_exps[g + 1] = old_exponents(loaded[g + 1])
             for h in range(GROUP // PAIR):
-                recurrence(g, h, loaded[g], packed[g], old_exps[g])
+                recurrence(g, h, loaded[g], packed[g])

@@ -19,8 +19,12 @@ TILES = ROWS // P
 GROUP = 4
 PAIR = 2
 GROUPS = TILES // GROUP
+PAIRS = TILES // PAIR
+STEPS = 2 * GROUPS
 GROUP_ROWS = GROUP * P
 QUADRANT = 32
+TOP, BOTTOM = 0, 1
+FIRST_SLOT = -4
 
 FLOPS = 2 * 2 * ROWS * E * D
 
@@ -61,34 +65,48 @@ def tile_rwkv_timemix_for_quant_pa_t_kernel(
 
     with ExitStack() as pools:
         const = pools.enter_context(tc.tile_pool(name="const", bufs=1))
-        loads = pools.enter_context(tc.tile_pool(name="loads", bufs=3))
+        rows_in = pools.enter_context(tc.tile_pool(name="rows_in", bufs=2))
+        states_in = pools.enter_context(tc.tile_pool(name="states_in", bufs=4))
         stage = pools.enter_context(tc.tile_pool(name="stage", bufs=1))
         operands = pools.enter_context(tc.tile_pool(name="operands", bufs=2))
-        work = pools.enter_context(tc.tile_pool(name="work", bufs=3))
+        work = pools.enter_context(tc.tile_pool(name="work", bufs=2))
         results = pools.enter_context(tc.tile_pool(name="results", bufs=3))
         psum_t = pools.enter_context(tc.psum_pool(name="psum_t", bufs=1))
         psum_kv = pools.enter_context(tc.psum_pool(name="psum_kv", bufs=2))
 
+        loaded = {}
+        planes_of = {}
+        prev_part = {}
+        mixed = {}
+        grouped = {}
+        operand = {}
+        acc = {}
+        gap = {}
+        lead = {}
+        old_w = {}
+        olds = {}
+        news = {}
+
         def load_group(g):
             tiles = slice(g * GROUP, (g + 1) * GROUP)
-            sx_sb = loads.tile([P, GROUP, E], BF16, name="sx_sb")
+            sx_sb = rows_in.tile([P, GROUP, E], BF16, name="sx_sb")
             nc.sync.dma_start(out=sx_sb[:], in_=sx_rows[:, tiles, :])
-            x_sb = loads.tile([P, GROUP, E], BF16, name="x_sb")
+            x_sb = rows_in.tile([P, GROUP, E], BF16, name="x_sb")
             nc.sync.dma_start(out=x_sb[:], in_=x_rows[:, tiles, :])
-            sp_sb = loads.tile([P, GROUP, D], BF16, name="sp_sb")
+            sp_sb = states_in.tile([P, GROUP, D], BF16, name="sp_sb")
             nc.sync.dma_start(out=sp_sb[:], in_=sp_rows[:, tiles, :])
-            sa_sb = loads.tile([P, GROUP, D], BF16, name="sa_sb")
+            sa_sb = states_in.tile([P, GROUP, D], BF16, name="sa_sb")
             nc.sync.dma_start(out=sa_sb[:], in_=sa_rows[:, tiles, :])
-            sb_sb = loads.tile([P, GROUP, D], BF16, name="sb_sb")
+            sb_sb = states_in.tile([P, GROUP, D], BF16, name="sb_sb")
             nc.sync.dma_start(out=sb_sb[:], in_=sb_rows[:, tiles, :])
-            return {"x": x_sb, "sx": sx_sb, "sp": sp_sb, "sa": sa_sb, "sb": sb_sb}
+            loaded[g] = {"x": x_sb, "sx": sx_sb, "sp": sp_sb, "sa": sa_sb, "sb": sb_sb}
 
         ident = const.tile([P, P], BF16, name="ident")
         make_identity(nc, ident[:])
 
         def load_mix(time_mix, label):
             raw = const.tile([P, PACK], BF16, name="mix_raw_" + label)
-            nc.sync.dma_start(out=raw[:], in_=time_mix.rearrange("o (p j) -> (o p) j", j=PACK))
+            nc.scalar.dma_start(out=raw[:], in_=time_mix.rearrange("o (p j) -> (o p) j", j=PACK))
             mix = const.tile([P, PACK], F32, name="mix_" + label)
             nc.vector.tensor_copy(out=mix[:], in_=raw[:])
             rest = const.tile([P, PACK], F32, name="rest_" + label)
@@ -114,87 +132,94 @@ def tile_rwkv_timemix_for_quant_pa_t_kernel(
 
         mix_k, rest_k = load_mix(time_mix_k, "k")
         mix_v, rest_v = load_mix(time_mix_v, "v")
-        loaded = {0: load_group(0)}
-        wk_codes, wk_plane = load_weight(W_key_words, W_key_scales, "k")
-        wv_codes, wv_plane = load_weight(W_value_words, W_value_scales, "v")
+        load_group(0)
+        weight_k = load_weight(W_key_words, W_key_scales, "k")
+        weight_v = load_weight(W_value_words, W_value_scales, "v")
+        streams = [("k", mix_k, rest_k, weight_k), ("v", mix_v, rest_v, weight_v)]
 
         tf_bf = const.tile([P, D], BF16, name="tf_bf")
-        nc.sync.dma_start(out=tf_bf[:], in_=time_first.partition_broadcast(P))
+        nc.scalar.dma_start(out=tf_bf[:], in_=time_first.partition_broadcast(P))
         td_bf = const.tile([P, D], BF16, name="td_bf")
-        nc.sync.dma_start(out=td_bf[:], in_=time_decay.partition_broadcast(P))
+        nc.scalar.dma_start(out=td_bf[:], in_=time_decay.partition_broadcast(P))
         decay = const.tile([P, D], F32, name="decay")
         nc.scalar.activation(out=decay[:], in_=td_bf[:], func=FUNC.Exp)
         shift = const.tile([P, 2, D], F32, name="shift")
         nc.vector.tensor_scalar_mul(out=shift[:, 0, :], in0=tf_bf[:], scalar1=-1.0)
         nc.vector.tensor_scalar_mul(out=shift[:, 1, :], in0=decay[:], scalar1=-1.0)
 
-        def transpose_two_planes(rows_sb, first_plane, label):
-            bank = psum_t.tile([P, 2, GROUP_ROWS], BF16, name="%s_t%d" % (label, first_plane))
-            for jj in range(2):
-                for i in range(GROUP):
-                    nc.tensor.transpose(
-                        out=bank[:, jj, i * P : (i + 1) * P],
-                        in_=rows_sb[:, i, first_plane + jj : E : PACK],
-                        identity=ident[:],
-                    )
-            return [bank[:, jj, :] for jj in range(2)]
-
-        def mix_and_quantise(group):
-            x_planes = []
-            sx_planes = []
+        def transpose_group(g, which):
+            planes = []
             for first_plane in range(0, PACK, 2):
-                sx_planes.extend(transpose_two_planes(group["sx"], first_plane, "sx"))
-                x_planes.extend(transpose_two_planes(group["x"], first_plane, "x"))
-            streams = [("k", mix_k, rest_k), ("v", mix_v, rest_v)]
-            prev_part = {}
-            mixed = {}
-            for label, mix, rest in streams:
-                prev_part[label] = stage.tile([P, PACK, GROUP_ROWS], F32, name="prev_part_" + label)
-                mixed[label] = stage.tile([P, PACK, GROUP_ROWS], BF16, name="mixed_" + label)
-            for label, mix, rest in streams:
-                for j in range(PACK):
-                    nc.scalar.activation(
-                        out=prev_part[label][:, j, :],
-                        in_=sx_planes[j],
-                        func=FUNC.Copy,
-                        scale=rest[:, j : j + 1],
-                    )
-            for label, mix, rest in streams:
-                for j in range(PACK):
-                    nc.vector.scalar_tensor_tensor(
-                        out=mixed[label][:, j, :],
-                        in0=x_planes[j],
-                        scalar=mix[:, j : j + 1],
-                        in1=prev_part[label][:, j, :],
-                        op0=ALU.mult,
-                        op1=ALU.add,
-                    )
-            packed = {}
-            for label, mix, rest in streams:
-                grouped = stage.tile(
-                    [P, GROUP_ROWS, PACK], BF16, name="grouped_" + label, align_bytes=64
-                )
-                nc.scalar.copy(
-                    out=grouped[:].rearrange("p (c i) j -> p c j i", i=4),
-                    in_=mixed[label][:].rearrange("p j (c i) -> p c j i", i=4),
-                )
-                codes = operands.tile([P, GROUP_ROWS], U32, name="codes_" + label, align_bytes=64)
-                plane = operands.tile([P, GROUP_ROWS], U8, name="plane_" + label, align_bytes=64)
-                nc.vector.quantize_mx(
-                    out=codes[:].bitcast(FP8X4),
-                    scales=plane[:],
-                    in_=grouped[:].rearrange("p r j -> p (r j)"),
-                )
-                packed[label] = (codes, plane)
-            return packed
+                bank = psum_t.tile([P, 2, GROUP_ROWS], BF16, name="%s_t%d" % (which, first_plane))
+                for jj in range(2):
+                    for i in range(GROUP):
+                        nc.tensor.transpose(
+                            out=bank[:, jj, i * P : (i + 1) * P],
+                            in_=loaded[g][which][:, i, first_plane + jj : E : PACK],
+                            identity=ident[:],
+                        )
+                    planes.append(bank[:, jj, :])
+            planes_of[(which, g)] = planes
 
-        def project(operand, w_codes, w_plane, first_tile, label):
-            codes, plane = operand
-            acc = psum_kv.tile([P, PAIR, D], F32, name="acc_" + label)
+        def transpose_prev(g):
+            transpose_group(g, "sx")
+
+        def transpose_cur(g):
+            transpose_group(g, "x")
+
+        def scale_prev(m):
+            label, mix, rest, weight = streams[m % 2]
+            prev_part[m] = stage.tile([P, PACK, GROUP_ROWS], F32, name="prev_part_" + label)
+            for j in range(PACK):
+                nc.scalar.activation(
+                    out=prev_part[m][:, j, :],
+                    in_=planes_of[("sx", m // 2)][j],
+                    func=FUNC.Copy,
+                    scale=rest[:, j : j + 1],
+                )
+
+        def mix_step(m):
+            label, mix, rest, weight = streams[m % 2]
+            mixed[m] = stage.tile([P, PACK, GROUP_ROWS], BF16, name="mixed_" + label)
+            for j in range(PACK):
+                nc.vector.scalar_tensor_tensor(
+                    out=mixed[m][:, j, :],
+                    in0=planes_of[("x", m // 2)][j],
+                    scalar=mix[:, j : j + 1],
+                    in1=prev_part[m][:, j, :],
+                    op0=ALU.mult,
+                    op1=ALU.add,
+                )
+
+        def regroup(m):
+            label = streams[m % 2][0]
+            grouped[m] = stage.tile([P, GROUP_ROWS, PACK], BF16, name="grouped_" + label, align_bytes=64)
+            nc.scalar.copy(
+                out=grouped[m][:].rearrange("p (c i) j -> p c j i", i=4),
+                in_=mixed[m][:].rearrange("p j (c i) -> p c j i", i=4),
+            )
+
+        def quantise(m):
+            label = streams[m % 2][0]
+            codes = operands.tile([P, GROUP_ROWS], U32, name="codes_" + label, align_bytes=64)
+            plane = operands.tile([P, GROUP_ROWS], U8, name="plane_" + label, align_bytes=64)
+            nc.vector.quantize_mx(
+                out=codes[:].bitcast(FP8X4),
+                scales=plane[:],
+                in_=grouped[m][:].rearrange("p r j -> p (r j)"),
+            )
+            operand[m] = (codes, plane)
+
+        def project(q, stream):
+            label, mix, rest, weight = streams[stream]
+            codes, plane = operand[2 * (q // 2) + stream]
+            w_codes, w_plane = weight
+            acc[(label, q)] = psum_kv.tile([P, PAIR, D], F32, name="acc_" + label)
             for i in range(PAIR):
-                cols = slice((first_tile + i) * P, (first_tile + i + 1) * P)
+                first_col = ((q % 2) * PAIR + i) * P
+                cols = slice(first_col, first_col + P)
                 nc.tensor.matmul_mx(
-                    out=acc[:, i, :],
+                    out=acc[(label, q)][:, i, :],
                     lhsT=codes[:, cols].bitcast(FP8X4),
                     lhsT_scale=plane[:, cols],
                     rhs=w_codes[:].bitcast(FP8X4),
@@ -202,86 +227,118 @@ def tile_rwkv_timemix_for_quant_pa_t_kernel(
                     start=True,
                     stop=True,
                 )
-            return acc
 
-        def recurrence(g, h, group, packed):
-            first_tile = h * PAIR
-            tiles = slice(first_tile, first_tile + PAIR)
-            out_tiles = slice(g * GROUP + first_tile, g * GROUP + first_tile + PAIR)
-            k_ps = project(packed["k"], wk_codes, wk_plane, first_tile, "k")
-            v_ps = project(packed["v"], wv_codes, wv_plane, first_tile, "v")
+        def project_k(q):
+            project(q, 0)
 
-            both = [P, 2, PAIR, D]
-            flat = [P, 2, PAIR * D]
+        def project_v(q):
+            project(q, 1)
 
-            def twice(ap):
-                return ap.rearrange("p i d -> p (i d)").unsqueeze(1).to_broadcast(flat)
+        both = [P, 2, PAIR, D]
+        flat = [P, 2, PAIR * D]
+        four = [P, 2, 2, PAIR, D]
 
-            def flat_view(tile_ap):
-                return tile_ap.rearrange("p w i d -> p w (i d)")
+        def state_of(q, which):
+            first_tile = (q % 2) * PAIR
+            return loaded[q // 2][which][:, first_tile : first_tile + PAIR, :]
 
-            gap = work.tile([P, PAIR, D], F32, name="gap")
-            nc.vector.tensor_tensor(out=gap[:], in0=group["sp"][:, tiles, :], in1=k_ps[:], op=ALU.subtract)
-            lead = work.tile(both, F32, name="lead")
+        def out_tiles(q):
+            return slice(q * PAIR, (q + 1) * PAIR)
+
+        def twice(ap):
+            return ap.rearrange("p i d -> p (i d)").unsqueeze(1).to_broadcast(flat)
+
+        def flat_view(tile_ap):
+            return tile_ap.rearrange("p w i d -> p w (i d)")
+
+        def gap_of(q):
+            gap[q] = work.tile([P, PAIR, D], F32, name="gap")
             nc.vector.tensor_tensor(
-                out=lead[:],
-                in0=gap[:].unsqueeze(1).to_broadcast(both),
+                out=gap[q][:], in0=state_of(q, "sp"), in1=acc[("k", q)][:], op=ALU.subtract
+            )
+
+        def lead_of(q):
+            lead[q] = work.tile(both, F32, name="lead")
+            nc.vector.tensor_tensor(
+                out=lead[q][:],
+                in0=gap[q][:].unsqueeze(1).to_broadcast(both),
                 in1=shift[:].unsqueeze(2).to_broadcast(both),
                 op=ALU.add,
             )
+
+        def new_exponent(q):
             new_p = results.tile([P, PAIR, D], F32, name="new_p")
             nc.vector.scalar_tensor_tensor(
                 out=new_p[:].rearrange("p i d -> p (i d)"),
-                in0=lead[:, 1, :, :].rearrange("p i d -> p (i d)"),
+                in0=lead[q][:, 1, :, :].rearrange("p i d -> p (i d)"),
                 scalar=0.0,
-                in1=k_ps[:].rearrange("p i d -> p (i d)"),
+                in1=acc[("k", q)][:].rearrange("p i d -> p (i d)"),
                 op0=ALU.max,
                 op1=ALU.add,
             )
-            nc.sync.dma_start(out=new_p_rows[:, out_tiles, :], in_=new_p[:])
-            old_w = work.tile(both, F32, name="old_w")
-            nc.scalar.activation(out=old_w[:], in_=lead[:], func=FUNC.Exp)
+            nc.sync.dma_start(out=new_p_rows[:, out_tiles(q), :], in_=new_p[:])
+
+        def weights(q):
             excess = work.tile(both, F32, name="excess")
-            nc.scalar.activation(out=excess[:], in_=lead[:], func=FUNC.Relu)
-            new_w = work.tile(both, F32, name="new_w")
-            nc.scalar.activation(out=new_w[:], in_=excess[:], func=FUNC.Exp, scale=-1.0)
+            nc.scalar.activation(out=excess[:], in_=lead[q][:], func=FUNC.Relu)
+            news[q] = work.tile(four, F32, name="news")
+            nc.scalar.activation(out=news[q][:, BOTTOM], in_=excess[:], func=FUNC.Exp, scale=-1.0)
+            old_w[q] = work.tile(both, F32, name="old_w")
+            nc.scalar.activation(out=old_w[q][:], in_=lead[q][:], func=FUNC.Exp)
 
-            old_b = work.tile(both, F32, name="old_b")
-            nc.vector.scalar_tensor_tensor(
-                out=flat_view(old_b[:]), in0=flat_view(old_w[:]), scalar=1.0,
-                in1=twice(group["sb"][:, tiles, :]), op0=ALU.min, op1=ALU.mult,
-            )
-            old_a = work.tile(both, F32, name="old_a")
-            nc.vector.scalar_tensor_tensor(
-                out=flat_view(old_a[:]), in0=flat_view(old_w[:]), scalar=1.0,
-                in1=twice(group["sa"][:, tiles, :]), op0=ALU.min, op1=ALU.mult,
-            )
-            new_a = work.tile(both, F32, name="new_a")
+        def new_term(q):
             nc.vector.tensor_tensor(
-                out=flat_view(new_a[:]), in0=flat_view(new_w[:]), in1=twice(v_ps[:]), op=ALU.mult
+                out=flat_view(news[q][:, TOP]), in0=flat_view(news[q][:, BOTTOM]),
+                in1=twice(acc[("v", q)][:]), op=ALU.mult,
             )
-            sum_b = results.tile(both, F32, name="sum_b")
-            sum_a = results.tile(both, F32, name="sum_a")
-            for w in range(2):
-                nc.gpsimd.tensor_tensor(
-                    out=sum_b[:, w, :, :], in0=old_b[:, w, :, :], in1=new_w[:, w, :, :], op=ALU.add
-                )
-            for w in range(2):
-                nc.gpsimd.tensor_tensor(
-                    out=sum_a[:, w, :, :], in0=old_a[:, w, :, :], in1=new_a[:, w, :, :], op=ALU.add
-                )
 
-            nc.sync.dma_start(out=b_rows[:, out_tiles, :], in_=sum_b[:, 0, :, :])
-            nc.sync.dma_start(out=new_b_rows[:, out_tiles, :], in_=sum_b[:, 1, :, :])
-            nc.sync.dma_start(out=a_rows[:, out_tiles, :], in_=sum_a[:, 0, :, :])
-            nc.sync.dma_start(out=new_a_rows[:, out_tiles, :], in_=sum_a[:, 1, :, :])
+        def old_b_term(q):
+            olds[q] = work.tile(four, F32, name="olds")
+            nc.vector.scalar_tensor_tensor(
+                out=flat_view(olds[q][:, BOTTOM]), in0=flat_view(old_w[q][:]), scalar=1.0,
+                in1=twice(state_of(q, "sb")), op0=ALU.min, op1=ALU.mult,
+            )
 
-        loaded[1] = load_group(1)
-        packed = {0: mix_and_quantise(loaded[0])}
-        for g in range(GROUPS):
-            if g + 2 < GROUPS:
-                loaded[g + 2] = load_group(g + 2)
-            if g + 1 < GROUPS:
-                packed[g + 1] = mix_and_quantise(loaded[g + 1])
-            for h in range(GROUP // PAIR):
-                recurrence(g, h, loaded[g], packed[g])
+        def old_a_term(q):
+            nc.vector.scalar_tensor_tensor(
+                out=flat_view(olds[q][:, TOP]), in0=flat_view(old_w[q][:]), scalar=1.0,
+                in1=twice(state_of(q, "sa")), op0=ALU.min, op1=ALU.mult,
+            )
+
+        def sums(q):
+            total = results.tile(four, F32, name="total")
+            nc.gpsimd.tensor_tensor(out=total[:], in0=olds[q][:], in1=news[q][:], op=ALU.add)
+            nc.sync.dma_start(out=a_rows[:, out_tiles(q), :], in_=total[:, TOP, 0])
+            nc.sync.dma_start(out=new_a_rows[:, out_tiles(q), :], in_=total[:, TOP, 1])
+            nc.sync.dma_start(out=b_rows[:, out_tiles(q), :], in_=total[:, BOTTOM, 0])
+            nc.sync.dma_start(out=new_b_rows[:, out_tiles(q), :], in_=total[:, BOTTOM, 1])
+
+        def run(stage_of, index, count):
+            if 0 <= index < count:
+                stage_of(index)
+
+        def slot(s):
+            run(new_term, s, PAIRS)
+            run(regroup, s + 2, STEPS)
+            run(lead_of, s + 1, PAIRS)
+            run(old_b_term, s, PAIRS)
+            run(quantise, s + 2, STEPS)
+            run(project_k, s + 2, PAIRS)
+            run(project_v, s + 1, PAIRS)
+            run(old_a_term, s, PAIRS)
+            run(sums, s, PAIRS)
+            run(scale_prev, s + 3, STEPS)
+            run(weights, s + 1, PAIRS)
+            run(new_exponent, s + 1, PAIRS)
+            run(gap_of, s + 2, PAIRS)
+            run(mix_step, s + 3, STEPS)
+            if s % 2 == 0:
+                run(transpose_prev, (s + 4) // 2, GROUPS)
+                run(transpose_cur, (s + 4) // 2, GROUPS)
+                run(load_group, (s + 6) // 2, GROUPS)
+
+        for s in range(FIRST_SLOT, 0):
+            slot(s)
+        with tc.manual_schedule():
+            for s in range(PAIRS):
+                slot(s)

@@ -307,7 +307,8 @@ def tile_rwkv_timemix_for_quant_pa_t_kernel(
 
         def sums(q):
             total = results.tile(four, F32, name="total")
-            nc.gpsimd.tensor_tensor(out=total[:], in0=olds[q][:], in1=news[q][:], op=ALU.add)
+            adder = nc.vector if q == PAIRS - 1 else nc.gpsimd
+            adder.tensor_tensor(out=total[:], in0=olds[q][:], in1=news[q][:], op=ALU.add)
             nc.sync.dma_start(out=a_rows[:, out_tiles(q), :], in_=total[:, TOP, 0])
             nc.sync.dma_start(out=new_a_rows[:, out_tiles(q), :], in_=total[:, TOP, 1])
             nc.sync.dma_start(out=b_rows[:, out_tiles(q), :], in_=total[:, BOTTOM, 0])

@@ -72,7 +72,9 @@ def tile_rwkv_timemix_for_quant_pa_t_kernel(
         work = pools.enter_context(tc.tile_pool(name="work", bufs=2))
         results = pools.enter_context(tc.tile_pool(name="results", bufs=3))
         psum_t = pools.enter_context(tc.psum_pool(name="psum_t", bufs=1))
-        psum_kv = pools.enter_context(tc.psum_pool(name="psum_kv", bufs=2))
+        psum_k = pools.enter_context(tc.psum_pool(name="psum_k", bufs=2))
+        psum_v = pools.enter_context(tc.psum_pool(name="psum_v", bufs=1))
+        psum_c = pools.enter_context(tc.psum_pool(name="psum_c", bufs=1))
 
         loaded = {}
         planes_of = {}
@@ -103,6 +105,8 @@ def tile_rwkv_timemix_for_quant_pa_t_kernel(
 
         ident = const.tile([P, P], BF16, name="ident")
         make_identity(nc, ident[:])
+        ident_f = const.tile([P, P], F32, name="ident_f")
+        make_identity(nc, ident_f[:])
 
         def load_mix(time_mix, label):
             raw = const.tile([P, PACK], BF16, name="mix_raw_" + label)
@@ -137,15 +141,24 @@ def tile_rwkv_timemix_for_quant_pa_t_kernel(
         weight_v = load_weight(W_value_words, W_value_scales, "v")
         streams = [("k", mix_k, rest_k, weight_k), ("v", mix_v, rest_v, weight_v)]
 
-        tf_bf = const.tile([P, D], BF16, name="tf_bf")
-        nc.scalar.dma_start(out=tf_bf[:], in_=time_first.partition_broadcast(P))
-        td_bf = const.tile([P, D], BF16, name="td_bf")
-        nc.scalar.dma_start(out=td_bf[:], in_=time_decay.partition_broadcast(P))
-        decay = const.tile([P, D], F32, name="decay")
-        nc.scalar.activation(out=decay[:], in_=td_bf[:], func=FUNC.Exp)
-        shift = const.tile([P, 2, D], F32, name="shift")
-        nc.vector.tensor_scalar_mul(out=shift[:, 0, :], in0=tf_bf[:], scalar1=-1.0)
-        nc.vector.tensor_scalar_mul(out=shift[:, 1, :], in0=decay[:], scalar1=-1.0)
+        halves = D // P
+        tf_col = const.tile([P, halves, 2], BF16, name="tf_col")
+        nc.scalar.dma_start(out=tf_col[:, :, 0:1], in_=time_first.rearrange("(h p o) -> p h o", p=P, o=1))
+        td_col = const.tile([P, halves, 2], BF16, name="td_col")
+        nc.scalar.dma_start(out=td_col[:, :, 0:1], in_=time_decay.rearrange("(h p o) -> p h o", p=P, o=1))
+        decay = const.tile([P, halves], F32, name="decay")
+        nc.scalar.activation(out=decay[:], in_=td_col[:, :, 0], func=FUNC.Exp)
+        shift_col = const.tile([P, 2, halves], F32, name="shift_col")
+        nc.vector.tensor_scalar_mul(out=shift_col[:, 0, :], in0=tf_col[:, :, 0], scalar1=-1.0)
+        nc.vector.tensor_scalar_mul(out=shift_col[:, 1, :], in0=decay[:], scalar1=-1.0)
+        shift = psum_c.tile([P, 2, D], F32, name="shift")
+        for w in range(2):
+            for h in range(halves):
+                nc.tensor.transpose(
+                    out=shift[:, w, h * P : (h + 1) * P],
+                    in_=shift_col[:, w, h : h + 1].to_broadcast([P, P]),
+                    identity=ident_f[:],
+                )
 
         def transpose_group(g, which):
             planes = []
@@ -214,7 +227,7 @@ def tile_rwkv_timemix_for_quant_pa_t_kernel(
             label, mix, rest, weight = streams[stream]
             codes, plane = operand[2 * (q // 2) + stream]
             w_codes, w_plane = weight
-            acc[(label, q)] = psum_kv.tile([P, PAIR, D], F32, name="acc_" + label)
+            acc[(label, q)] = (psum_k, psum_v)[stream].tile([P, PAIR, D], F32, name="acc_" + label)
             for i in range(PAIR):
                 first_col = ((q % 2) * PAIR + i) * P
                 cols = slice(first_col, first_col + P)

@@ -25,6 +25,7 @@ GROUP_ROWS = GROUP * P
 QUADRANT = 32
 TOP, BOTTOM = 0, 1
 FIRST_SLOT = -4
+DRAIN = PAIRS - 3
 
 FLOPS = 2 * 2 * ROWS * E * D
 
@@ -88,6 +89,9 @@ def tile_rwkv_timemix_for_quant_pa_t_kernel(
         old_w = {}
         olds = {}
         news = {}
+        flipped_ps = {}
+        flipped_sb = {}
+        states_ps = {}
 
         def load_group(g):
             tiles = slice(g * GROUP, (g + 1) * GROUP)
@@ -255,6 +259,42 @@ def tile_rwkv_timemix_for_quant_pa_t_kernel(
             first_tile = (q % 2) * PAIR
             return loaded[q // 2][which][:, first_tile : first_tile + PAIR, :]
 
+        halves_of = [P, 2, PAIR, D // P, P]
+
+        def bank_of(q, back):
+            return ("sx_t%d" if (q - DRAIN) % 2 == 0 else "x_t%d") % (2 if back else 0)
+
+        def flip_states(q):
+            flipped_ps[q] = psum_t.tile(halves_of, BF16, name=bank_of(q, False))
+            for part, which in ((TOP, "sa"), (BOTTOM, "sb")):
+                for i in range(PAIR):
+                    for h in range(D // P):
+                        nc.tensor.transpose(
+                            out=flipped_ps[q][:, part, i, h, :],
+                            in_=state_of(q, which)[:, i, h * P : (h + 1) * P],
+                            identity=ident[:],
+                        )
+
+        def keep_flipped(q):
+            flipped_sb[q] = work.tile(halves_of, BF16, name="flipped_sb")
+            nc.scalar.copy(out=flipped_sb[q][:], in_=flipped_ps[q][:])
+
+        def flip_back(q):
+            states_ps[q] = psum_t.tile([P, 2, PAIR, D], BF16, name=bank_of(q, True))
+            for part in (TOP, BOTTOM):
+                for i in range(PAIR):
+                    for h in range(D // P):
+                        nc.tensor.transpose(
+                            out=states_ps[q][:, part, i, h * P : (h + 1) * P],
+                            in_=flipped_sb[q][:, part, i, h, :],
+                            identity=ident[:],
+                        )
+
+        def state_factor(q, part):
+            if q >= DRAIN:
+                return states_ps[q][:, part]
+            return state_of(q, ("sa", "sb")[part])
+
         def out_tiles(q):
             return slice(q * PAIR, (q + 1) * PAIR)
 
@@ -309,13 +349,13 @@ def tile_rwkv_timemix_for_quant_pa_t_kernel(
             olds[q] = work.tile(four, F32, name="olds")
             nc.vector.scalar_tensor_tensor(
                 out=flat_view(olds[q][:, BOTTOM]), in0=flat_view(old_w[q][:]), scalar=1.0,
-                in1=twice(state_of(q, "sb")), op0=ALU.min, op1=ALU.mult,
+                in1=twice(state_factor(q, BOTTOM)), op0=ALU.min, op1=ALU.mult,
             )
 
         def old_a_term(q):
             nc.vector.scalar_tensor_tensor(
                 out=flat_view(olds[q][:, TOP]), in0=flat_view(old_w[q][:]), scalar=1.0,
-                in1=twice(state_of(q, "sa")), op0=ALU.min, op1=ALU.mult,
+                in1=twice(state_factor(q, TOP)), op0=ALU.min, op1=ALU.mult,
             )
 
         def sums(q):
@@ -342,6 +382,10 @@ def tile_rwkv_timemix_for_quant_pa_t_kernel(
             run(old_a_term, s, PAIRS)
             run(sums, s, PAIRS)
             run(scale_prev, s + 3, STEPS)
+            if s + 1 >= DRAIN:
+                run(flip_states, s + 1, PAIRS)
+                run(keep_flipped, s + 1, PAIRS)
+                run(flip_back, s + 1, PAIRS)
             run(weights, s + 1, PAIRS)
             run(new_exponent, s + 1, PAIRS)
             run(gap_of, s + 2, PAIRS)

@@ -25,7 +25,7 @@ GROUP_ROWS = GROUP * P
 QUADRANT = 32
 TOP, BOTTOM = 0, 1
 FIRST_SLOT = -4
-DRAIN = PAIRS - 3
+DRAIN = PAIRS - 2
 
 FLOPS = 2 * 2 * ROWS * E * D
 
@@ -382,8 +382,9 @@ def tile_rwkv_timemix_for_quant_pa_t_kernel(
             run(old_a_term, s, PAIRS)
             run(sums, s, PAIRS)
             run(scale_prev, s + 3, STEPS)
+            if s + 2 >= DRAIN:
+                run(flip_states, s + 2, PAIRS)
             if s + 1 >= DRAIN:
-                run(flip_states, s + 1, PAIRS)
                 run(keep_flipped, s + 1, PAIRS)
                 run(flip_back, s + 1, PAIRS)
             run(weights, s + 1, PAIRS)

@@ -93,12 +93,22 @@ def tile_rwkv_timemix_for_quant_pa_t_kernel(
         flipped_sb = {}
         states_ps = {}
 
+        def load_rows(g, rows, label):
+            if g == 0:
+                views = []
+                for i in range(GROUP):
+                    first = const.tile([P, E], BF16, name="first_%s_%d" % (label, i))
+                    nc.sync.dma_start(out=first[:], in_=rows[:, i, :])
+                    views.append(first[:])
+                return views
+            whole = rows_in.tile([P, GROUP, E], BF16, name=label + "_sb")
+            nc.sync.dma_start(out=whole[:], in_=rows[:, g * GROUP : (g + 1) * GROUP, :])
+            return [whole[:, i, :] for i in range(GROUP)]
+
         def load_group(g):
             tiles = slice(g * GROUP, (g + 1) * GROUP)
-            sx_sb = rows_in.tile([P, GROUP, E], BF16, name="sx_sb")
-            nc.sync.dma_start(out=sx_sb[:], in_=sx_rows[:, tiles, :])
-            x_sb = rows_in.tile([P, GROUP, E], BF16, name="x_sb")
-            nc.sync.dma_start(out=x_sb[:], in_=x_rows[:, tiles, :])
+            sx_sb = load_rows(g, sx_rows, "sx")
+            x_sb = load_rows(g, x_rows, "x")
             sp_sb = states_in.tile([P, GROUP, D], BF16, name="sp_sb")
             nc.sync.dma_start(out=sp_sb[:], in_=sp_rows[:, tiles, :])
             sa_sb = states_in.tile([P, GROUP, D], BF16, name="sa_sb")
@@ -165,17 +175,21 @@ def tile_rwkv_timemix_for_quant_pa_t_kernel(
                 )
 
         def transpose_group(g, which):
-            planes = []
-            for first_plane in range(0, PACK, 2):
-                bank = psum_t.tile([P, 2, GROUP_ROWS], BF16, name="%s_t%d" % (which, first_plane))
-                for jj in range(2):
-                    for i in range(GROUP):
-                        nc.tensor.transpose(
-                            out=bank[:, jj, i * P : (i + 1) * P],
-                            in_=loaded[g][which][:, i, first_plane + jj : E : PACK],
-                            identity=ident[:],
-                        )
-                    planes.append(bank[:, jj, :])
+            banks = [
+                psum_t.tile([P, 2, GROUP_ROWS], BF16, name="%s_t%d" % (which, first_plane))
+                for first_plane in range(0, PACK, 2)
+            ]
+            if g == 0:
+                order = [(i, j) for i in range(GROUP) for j in range(PACK)]
+            else:
+                order = [(i, j) for j in range(PACK) for i in range(GROUP)]
+            for i, j in order:
+                nc.tensor.transpose(
+                    out=banks[j // 2][:, j % 2, i * P : (i + 1) * P],
+                    in_=loaded[g][which][i][:, j:E:PACK],
+                    identity=ident[:],
+                )
+            planes = [banks[j // 2][:, j % 2, :] for j in range(PACK)]
             planes_of[(which, g)] = planes
 
         def transpose_prev(g):
@@ -358,14 +372,33 @@ def tile_rwkv_timemix_for_quant_pa_t_kernel(
                 in1=twice(state_factor(q, TOP)), op0=ALU.min, op1=ALU.mult,
             )
 
+        stores = {
+            (TOP, 0): a_rows, (TOP, 1): new_a_rows, (BOTTOM, 0): b_rows, (BOTTOM, 1): new_b_rows,
+        }
+
         def sums(q):
+            if q == PAIRS - 1:
+                for part in (BOTTOM, TOP):
+                    for w in range(2):
+                        last = const.tile([P, PAIR, D], F32, name="last_total_%d_%d" % (part, w))
+                        nc.vector.tensor_tensor(
+                            out=last[:], in0=olds[q][:, part, w], in1=news[q][:, part, w], op=ALU.add
+                        )
+                        nc.sync.dma_start(out=stores[(part, w)][:, out_tiles(q), :], in_=last[:])
+                return
             total = results.tile(four, F32, name="total")
-            adder = nc.vector if q == PAIRS - 1 else nc.gpsimd
-            adder.tensor_tensor(out=total[:], in0=olds[q][:], in1=news[q][:], op=ALU.add)
-            nc.sync.dma_start(out=a_rows[:, out_tiles(q), :], in_=total[:, TOP, 0])
-            nc.sync.dma_start(out=new_a_rows[:, out_tiles(q), :], in_=total[:, TOP, 1])
-            nc.sync.dma_start(out=b_rows[:, out_tiles(q), :], in_=total[:, BOTTOM, 0])
-            nc.sync.dma_start(out=new_b_rows[:, out_tiles(q), :], in_=total[:, BOTTOM, 1])
+            if q == PAIRS - 2:
+                for part in (BOTTOM, TOP):
+                    nc.gpsimd.tensor_tensor(
+                        out=total[:, part], in0=olds[q][:, part], in1=news[q][:, part], op=ALU.add
+                    )
+                    for w in range(2):
+                        nc.sync.dma_start(out=stores[(part, w)][:, out_tiles(q), :], in_=total[:, part, w])
+                return
+            nc.gpsimd.tensor_tensor(out=total[:], in0=olds[q][:], in1=news[q][:], op=ALU.add)
+            for part in (TOP, BOTTOM):
+                for w in range(2):
+                    nc.sync.dma_start(out=stores[(part, w)][:, out_tiles(q), :], in_=total[:, part, w])
 
         def run(stage_of, index, count):
             if 0 <= index < count:

@@ -89,8 +89,6 @@ def tile_rwkv_timemix_for_quant_pa_t_kernel(
         old_w = {}
         olds = {}
         news = {}
-        flipped_ps = {}
-        flipped_sb = {}
         states_ps = {}
 
         def load_rows(g, rows, label):
@@ -273,36 +271,16 @@ def tile_rwkv_timemix_for_quant_pa_t_kernel(
             first_tile = (q % 2) * PAIR
             return loaded[q // 2][which][:, first_tile : first_tile + PAIR, :]
 
-        halves_of = [P, 2, PAIR, D // P, P]
-
-        def bank_of(q, back):
-            return ("sx_t%d" if (q - DRAIN) % 2 == 0 else "x_t%d") % (2 if back else 0)
-
-        def flip_states(q):
-            flipped_ps[q] = psum_t.tile(halves_of, BF16, name=bank_of(q, False))
+        def states_to_psum(q):
+            states_ps[q] = psum_t.tile([P, 2, PAIR, D], BF16, name="sx_t%d" % (2 * (q - DRAIN)))
             for part, which in ((TOP, "sa"), (BOTTOM, "sb")):
-                for i in range(PAIR):
-                    for h in range(D // P):
-                        nc.tensor.transpose(
-                            out=flipped_ps[q][:, part, i, h, :],
-                            in_=state_of(q, which)[:, i, h * P : (h + 1) * P],
-                            identity=ident[:],
-                        )
-
-        def keep_flipped(q):
-            flipped_sb[q] = work.tile(halves_of, BF16, name="flipped_sb")
-            nc.scalar.copy(out=flipped_sb[q][:], in_=flipped_ps[q][:])
-
-        def flip_back(q):
-            states_ps[q] = psum_t.tile([P, 2, PAIR, D], BF16, name=bank_of(q, True))
-            for part in (TOP, BOTTOM):
-                for i in range(PAIR):
-                    for h in range(D // P):
-                        nc.tensor.transpose(
-                            out=states_ps[q][:, part, i, h * P : (h + 1) * P],
-                            in_=flipped_sb[q][:, part, i, h, :],
-                            identity=ident[:],
-                        )
+                nc.tensor.matmul(
+                    out=states_ps[q][:, part].rearrange("p i d -> p (i d)"),
+                    lhsT=ident[:],
+                    rhs=state_of(q, which).rearrange("p i d -> p (i d)"),
+                    start=True,
+                    stop=True,
+                )
 
         def state_factor(q, part):
             if q >= DRAIN:
@@ -415,11 +393,8 @@ def tile_rwkv_timemix_for_quant_pa_t_kernel(
             run(old_a_term, s, PAIRS)
             run(sums, s, PAIRS)
             run(scale_prev, s + 3, STEPS)
-            if s + 2 >= DRAIN:
-                run(flip_states, s + 2, PAIRS)
             if s + 1 >= DRAIN:
-                run(keep_flipped, s + 1, PAIRS)
-                run(flip_back, s + 1, PAIRS)
+                run(states_to_psum, s + 1, PAIRS)
             run(weights, s + 1, PAIRS)
             run(new_exponent, s + 1, PAIRS)
             run(gap_of, s + 2, PAIRS)

@@ -91,22 +91,28 @@ def tile_rwkv_timemix_for_quant_pa_t_kernel(
         news = {}
         states_ps = {}
 
+        def load_first(rows, label, i):
+            first = const.tile([P, E], BF16, name="first_%s_%d" % (label, i))
+            nc.sync.dma_start(out=first[:], in_=rows[:, i, :])
+            return first[:]
+
         def load_rows(g, rows, label):
-            if g == 0:
-                views = []
-                for i in range(GROUP):
-                    first = const.tile([P, E], BF16, name="first_%s_%d" % (label, i))
-                    nc.sync.dma_start(out=first[:], in_=rows[:, i, :])
-                    views.append(first[:])
-                return views
             whole = rows_in.tile([P, GROUP, E], BF16, name=label + "_sb")
             nc.sync.dma_start(out=whole[:], in_=rows[:, g * GROUP : (g + 1) * GROUP, :])
             return [whole[:, i, :] for i in range(GROUP)]
 
         def load_group(g):
             tiles = slice(g * GROUP, (g + 1) * GROUP)
-            sx_sb = load_rows(g, sx_rows, "sx")
-            x_sb = load_rows(g, x_rows, "x")
+            if g == 0:
+                sx_sb, x_sb = [], []
+                for half in range(2):
+                    for i in (2 * half, 2 * half + 1):
+                        sx_sb.append(load_first(sx_rows, "sx", i))
+                    for i in (2 * half, 2 * half + 1):
+                        x_sb.append(load_first(x_rows, "x", i))
+            else:
+                sx_sb = load_rows(g, sx_rows, "sx")
+                x_sb = load_rows(g, x_rows, "x")
             sp_sb = states_in.tile([P, GROUP, D], BF16, name="sp_sb")
             nc.sync.dma_start(out=sp_sb[:], in_=sp_rows[:, tiles, :])
             sa_sb = states_in.tile([P, GROUP, D], BF16, name="sa_sb")
@@ -177,10 +183,7 @@ def tile_rwkv_timemix_for_quant_pa_t_kernel(
                 psum_t.tile([P, 2, GROUP_ROWS], BF16, name="%s_t%d" % (which, first_plane))
                 for first_plane in range(0, PACK, 2)
             ]
-            if g == 0:
-                order = [(i, j) for i in range(GROUP) for j in range(PACK)]
-            else:
-                order = [(i, j) for j in range(PACK) for i in range(GROUP)]
+            order = [(i, j) for j in range(PACK) for i in range(GROUP)]
             for i, j in order:
                 nc.tensor.transpose(
                     out=banks[j // 2][:, j % 2, i * P : (i + 1) * P],
@@ -188,42 +191,67 @@ def tile_rwkv_timemix_for_quant_pa_t_kernel(
                     identity=ident[:],
                 )
             planes = [banks[j // 2][:, j % 2, :] for j in range(PACK)]
-            planes_of[(which, g)] = planes
+            planes_of[(which, g)] = [(slice(0, GROUP_ROWS), planes)]
+
+        def transpose_first_group():
+            half_rows = GROUP_ROWS // 2
+            planes_of[("sx", 0)] = []
+            planes_of[("x", 0)] = []
+            for half in range(2):
+                for which in ("sx", "x"):
+                    bank = psum_t.tile([P, PACK, half_rows], BF16, name="%s_t%d" % (which, 2 * half))
+                    for i in range(2):
+                        for j in range(PACK):
+                            nc.tensor.transpose(
+                                out=bank[:, j, i * P : (i + 1) * P],
+                                in_=loaded[0][which][2 * half + i][:, j:E:PACK],
+                                identity=ident[:],
+                            )
+                    planes_of[(which, 0)].append(
+                        (slice(half * half_rows, (half + 1) * half_rows), [bank[:, j, :] for j in range(PACK)])
+                    )
 
         def transpose_prev(g):
-            transpose_group(g, "sx")
+            if g == 0:
+                transpose_first_group()
+            else:
+                transpose_group(g, "sx")
 
         def transpose_cur(g):
-            transpose_group(g, "x")
+            if g > 0:
+                transpose_group(g, "x")
 
         def scale_prev(m):
             label, mix, rest, weight = streams[m % 2]
             prev_part[m] = stage.tile([P, PACK, GROUP_ROWS], F32, name="prev_part_" + label)
-            for j in range(PACK):
-                nc.scalar.activation(
-                    out=prev_part[m][:, j, :],
-                    in_=planes_of[("sx", m // 2)][j],
-                    func=FUNC.Copy,
-                    scale=rest[:, j : j + 1],
-                )
+            for rows, planes in planes_of[("sx", m // 2)]:
+                for j in range(PACK):
+                    nc.scalar.activation(
+                        out=prev_part[m][:, j, rows],
+                        in_=planes[j],
+                        func=FUNC.Copy,
+                        scale=rest[:, j : j + 1],
+                    )
 
         def mix_step(m):
             label, mix, rest, weight = streams[m % 2]
             mixed[m] = stage.tile([P, PACK, GROUP_ROWS], BF16, name="mixed_" + label)
-            for j in range(PACK):
-                nc.vector.scalar_tensor_tensor(
-                    out=mixed[m][:, j, :],
-                    in0=planes_of[("x", m // 2)][j],
-                    scalar=mix[:, j : j + 1],
-                    in1=prev_part[m][:, j, :],
-                    op0=ALU.mult,
-                    op1=ALU.add,
-                )
+            for rows, planes in planes_of[("x", m // 2)]:
+                for j in range(PACK):
+                    nc.vector.scalar_tensor_tensor(
+                        out=mixed[m][:, j, rows],
+                        in0=planes[j],
+                        scalar=mix[:, j : j + 1],
+                        in1=prev_part[m][:, j, rows],
+                        op0=ALU.mult,
+                        op1=ALU.add,
+                    )
 
         def regroup(m):
             label = streams[m % 2][0]
             grouped[m] = stage.tile([P, GROUP_ROWS, PACK], BF16, name="grouped_" + label, align_bytes=64)
-            nc.scalar.copy(
+            copier = nc.vector.tensor_copy if m < 2 else nc.scalar.copy
+            copier(
                 out=grouped[m][:].rearrange("p (c i) j -> p c j i", i=4),
                 in_=mixed[m][:].rearrange("p j (c i) -> p c j i", i=4),
             )

@@ -113,13 +113,35 @@ def tile_rwkv_timemix_for_quant_pa_t_kernel(
             else:
                 sx_sb = load_rows(g, sx_rows, "sx")
                 x_sb = load_rows(g, x_rows, "x")
-            sp_sb = states_in.tile([P, GROUP, D], BF16, name="sp_sb")
-            nc.sync.dma_start(out=sp_sb[:], in_=sp_rows[:, tiles, :])
-            sa_sb = states_in.tile([P, GROUP, D], BF16, name="sa_sb")
-            nc.sync.dma_start(out=sa_sb[:], in_=sa_rows[:, tiles, :])
-            sb_sb = states_in.tile([P, GROUP, D], BF16, name="sb_sb")
-            nc.sync.dma_start(out=sb_sb[:], in_=sb_rows[:, tiles, :])
-            loaded[g] = {"x": x_sb, "sx": sx_sb, "sp": sp_sb, "sa": sa_sb, "sb": sb_sb}
+            loaded[g] = {"x": x_sb, "sx": sx_sb}
+            load_state(g, "sp", sp_rows)
+            load_state(g, "sa", sa_rows)
+            load_state(g, "sb", sb_rows)
+
+        def load_state(g, which, rows):
+            state_sb = states_in.tile([P, GROUP, D], BF16, name=which + "_sb")
+            nc.sync.dma_start(out=state_sb[:], in_=rows[:, g * GROUP : (g + 1) * GROUP, :])
+            loaded[g][which] = state_sb
+
+        def load_head():
+            sx_sb, x_sb = [], []
+            for half in range(2):
+                for i in (2 * half, 2 * half + 1):
+                    sx_sb.append(load_first(sx_rows, "sx", i))
+                for i in (2 * half, 2 * half + 1):
+                    x_sb.append(load_first(x_rows, "x", i))
+            loaded[0] = {"x": x_sb, "sx": sx_sb}
+            loaded[1] = {"sx": load_rows(1, sx_rows, "sx")}
+            head_k = load_weight(W_key_words, W_key_scales, "k")
+            load_state(0, "sp", sp_rows)
+            loaded[1]["x"] = load_rows(1, x_rows, "x")
+            head_v = load_weight(W_value_words, W_value_scales, "v")
+            load_state(0, "sa", sa_rows)
+            load_state(0, "sb", sb_rows)
+            load_state(1, "sp", sp_rows)
+            load_state(1, "sa", sa_rows)
+            load_state(1, "sb", sb_rows)
+            return head_k, head_v
 
         ident = const.tile([P, P], BF16, name="ident")
         make_identity(nc, ident[:])
@@ -154,9 +176,7 @@ def tile_rwkv_timemix_for_quant_pa_t_kernel(
 
         mix_k, rest_k = load_mix(time_mix_k, "k")
         mix_v, rest_v = load_mix(time_mix_v, "v")
-        load_group(0)
-        weight_k = load_weight(W_key_words, W_key_scales, "k")
-        weight_v = load_weight(W_value_words, W_value_scales, "v")
+        weight_k, weight_v = load_head()
         streams = [("k", mix_k, rest_k, weight_k), ("v", mix_v, rest_v, weight_v)]
 
         halves = D // P
@@ -430,7 +450,8 @@ def tile_rwkv_timemix_for_quant_pa_t_kernel(
             if s % 2 == 0:
                 run(transpose_prev, (s + 4) // 2, GROUPS)
                 run(transpose_cur, (s + 4) // 2, GROUPS)
-                run(load_group, (s + 6) // 2, GROUPS)
+                if (s + 6) // 2 >= 2:
+                    run(load_group, (s + 6) // 2, GROUPS)
 
         for s in range(FIRST_SLOT, 0):
             slot(s)

@@ -270,11 +270,16 @@ def tile_rwkv_timemix_for_quant_pa_t_kernel(
         def regroup(m):
             label = streams[m % 2][0]
             grouped[m] = stage.tile([P, GROUP_ROWS, PACK], BF16, name="grouped_" + label, align_bytes=64)
-            copier = nc.vector.tensor_copy if m < 2 else nc.scalar.copy
-            copier(
-                out=grouped[m][:].rearrange("p (c i) j -> p c j i", i=4),
-                in_=mixed[m][:].rearrange("p j (c i) -> p c j i", i=4),
-            )
+            out_view = grouped[m][:].rearrange("p (c i) j -> p c j i", i=4)
+            in_view = mixed[m][:].rearrange("p j (c i) -> p c j i", i=4)
+            if m == 0:
+                nc.vector.tensor_copy(out=out_view, in_=in_view)
+            elif m == 1:
+                nc.gpsimd.tensor_scalar(
+                    out=out_view, in0=in_view, scalar1=1.0, scalar2=0.0, op0=ALU.mult, op1=ALU.add
+                )
+            else:
+                nc.scalar.copy(out=out_view, in_=in_view)
 
         def quantise(m):
             label = streams[m % 2][0]

@@ -27,6 +27,7 @@ TOP, BOTTOM = 0, 1
 FIRST_SLOT = -4
 DRAIN = PAIRS - 2
 
+MAIN = 208
 FLOPS = 2 * 2 * ROWS * E * D
 
 
@@ -198,6 +199,9 @@ def tile_rwkv_timemix_for_quant_pa_t_kernel(
                     identity=ident_f[:],
                 )
 
+        shift_sb = const.tile([P, 2, D - MAIN], F32, name="shift_sb")
+        nc.scalar.copy(out=shift_sb[:], in_=shift[:, :, MAIN:D])
+
         def transpose_group(g, which):
             banks = [
                 psum_t.tile([P, 2, GROUP_ROWS], BF16, name="%s_t%d" % (which, first_plane))
@@ -358,9 +362,15 @@ def tile_rwkv_timemix_for_quant_pa_t_kernel(
         def lead_of(q):
             lead[q] = work.tile(both, F32, name="lead")
             nc.vector.tensor_tensor(
-                out=lead[q][:],
-                in0=gap[q][:].unsqueeze(1).to_broadcast(both),
-                in1=shift[:].unsqueeze(2).to_broadcast(both),
+                out=lead[q][:, :, :, 0:MAIN],
+                in0=gap[q][:, :, 0:MAIN].unsqueeze(1).to_broadcast([P, 2, PAIR, MAIN]),
+                in1=shift[:, :, 0:MAIN].unsqueeze(2).to_broadcast([P, 2, PAIR, MAIN]),
+                op=ALU.add,
+            )
+            nc.gpsimd.tensor_tensor(
+                out=lead[q][:, :, :, MAIN:D],
+                in0=gap[q][:, :, MAIN:D].unsqueeze(1).to_broadcast([P, 2, PAIR, D - MAIN]),
+                in1=shift_sb[:].unsqueeze(2).to_broadcast([P, 2, PAIR, D - MAIN]),
                 op=ALU.add,
             )
 

@@ -361,12 +361,15 @@ def tile_rwkv_timemix_for_quant_pa_t_kernel(
 
         def lead_of(q):
             lead[q] = work.tile(both, F32, name="lead")
+            main = D if q == PAIRS - 1 else MAIN
             nc.vector.tensor_tensor(
-                out=lead[q][:, :, :, 0:MAIN],
-                in0=gap[q][:, :, 0:MAIN].unsqueeze(1).to_broadcast([P, 2, PAIR, MAIN]),
-                in1=shift[:, :, 0:MAIN].unsqueeze(2).to_broadcast([P, 2, PAIR, MAIN]),
+                out=lead[q][:, :, :, 0:main],
+                in0=gap[q][:, :, 0:main].unsqueeze(1).to_broadcast([P, 2, PAIR, main]),
+                in1=shift[:, :, 0:main].unsqueeze(2).to_broadcast([P, 2, PAIR, main]),
                 op=ALU.add,
             )
+            if main == D:
+                return
             nc.gpsimd.tensor_tensor(
                 out=lead[q][:, :, :, MAIN:D],
                 in0=gap[q][:, :, MAIN:D].unsqueeze(1).to_broadcast([P, 2, PAIR, D - MAIN]),

@@ -453,18 +453,18 @@ def tile_rwkv_timemix_for_quant_pa_t_kernel(
             run(regroup, s + 2, STEPS)
             run(lead_of, s + 1, PAIRS)
             run(old_b_term, s, PAIRS)
+            run(old_a_term, s, PAIRS)
+            run(sums, s, PAIRS)
             run(quantise, s + 2, STEPS)
             run(project_k, s + 2, PAIRS)
             run(project_v, s + 1, PAIRS)
-            run(old_a_term, s, PAIRS)
-            run(sums, s, PAIRS)
             run(scale_prev, s + 3, STEPS)
             if s + 1 >= DRAIN:
                 run(states_to_psum, s + 1, PAIRS)
             run(weights, s + 1, PAIRS)
             run(new_exponent, s + 1, PAIRS)
-            run(gap_of, s + 2, PAIRS)
             run(mix_step, s + 3, STEPS)
+            run(gap_of, s + 2, PAIRS)
             if s % 2 == 0:
                 run(transpose_prev, (s + 4) // 2, GROUPS)
                 run(transpose_cur, (s + 4) // 2, GROUPS)

@@ -463,8 +463,12 @@ def tile_rwkv_timemix_for_quant_pa_t_kernel(
                 run(states_to_psum, s + 1, PAIRS)
             run(weights, s + 1, PAIRS)
             run(new_exponent, s + 1, PAIRS)
-            run(mix_step, s + 3, STEPS)
-            run(gap_of, s + 2, PAIRS)
+            if s < 0:
+                run(gap_of, s + 2, PAIRS)
+                run(mix_step, s + 3, STEPS)
+            else:
+                run(mix_step, s + 3, STEPS)
+                run(gap_of, s + 2, PAIRS)
             if s % 2 == 0:
                 run(transpose_prev, (s + 4) // 2, GROUPS)
                 run(transpose_cur, (s + 4) // 2, GROUPS)

from contextlib import ExitStack

import concourse.mybir as mybir
from concourse.masks import make_identity

BF16 = mybir.dt.bfloat16
F32 = mybir.dt.float32
I32 = mybir.dt.int32
U8 = mybir.dt.uint8
U32 = mybir.dt.uint32
FP8X4 = mybir.dt.float8_e4m3fn_x4
ALU = mybir.AluOpType
FUNC = mybir.ActivationFunctionType

P = 128
PACK = 4
ROWS, E, D = 4096, 512, 256
TILES = ROWS // P
GROUP = 4
PAIR = 2
GROUPS = TILES // GROUP
PAIRS = TILES // PAIR
STEPS = 2 * GROUPS
GROUP_ROWS = GROUP * P
QUADRANT = 32
TOP, BOTTOM = 0, 1
FIRST_SLOT = -4
DRAIN = PAIRS - 2

MAIN = 208
FLOPS = 2 * 2 * ROWS * E * D


def tile_rwkv_timemix_for_quant_pa_t_kernel(
    tc,
    x,
    state_A,
    state_B,
    state_p,
    state_x,
    time_decay,
    time_first,
    time_mix_k,
    time_mix_v,
    W_key_words,
    W_key_scales,
    W_value_words,
    W_value_scales,
    out_0,
    out_1,
    out_2,
    out_3,
    out_4,
):
    nc = tc.nc
    by_tile = "(p t) c -> p t c"
    x_rows = x.rearrange(by_tile, t=TILES)
    sx_rows = state_x.rearrange(by_tile, t=TILES)
    sp_rows = state_p.rearrange(by_tile, t=TILES)
    sa_rows = state_A.rearrange(by_tile, t=TILES)
    sb_rows = state_B.rearrange(by_tile, t=TILES)
    a_rows = out_0.rearrange(by_tile, t=TILES)
    b_rows = out_1.rearrange(by_tile, t=TILES)
    new_a_rows = out_2.rearrange(by_tile, t=TILES)
    new_b_rows = out_3.rearrange(by_tile, t=TILES)
    new_p_rows = out_4.rearrange(by_tile, t=TILES)

    with ExitStack() as pools:
        const = pools.enter_context(tc.tile_pool(name="const", bufs=1))
        rows_in = pools.enter_context(tc.tile_pool(name="rows_in", bufs=2))
        states_in = pools.enter_context(tc.tile_pool(name="states_in", bufs=4))
        stage = pools.enter_context(tc.tile_pool(name="stage", bufs=1))
        operands = pools.enter_context(tc.tile_pool(name="operands", bufs=2))
        work = pools.enter_context(tc.tile_pool(name="work", bufs=2))
        results = pools.enter_context(tc.tile_pool(name="results", bufs=3))
        psum_t = pools.enter_context(tc.psum_pool(name="psum_t", bufs=1))
        psum_k = pools.enter_context(tc.psum_pool(name="psum_k", bufs=2))
        psum_v = pools.enter_context(tc.psum_pool(name="psum_v", bufs=1))
        psum_c = pools.enter_context(tc.psum_pool(name="psum_c", bufs=1))

        loaded = {}
        planes_of = {}
        prev_part = {}
        mixed = {}
        grouped = {}
        operand = {}
        acc = {}
        gap = {}
        lead = {}
        old_w = {}
        olds = {}
        news = {}
        states_ps = {}

        def load_first(rows, label, i):
            first = const.tile([P, E], BF16, name="first_%s_%d" % (label, i))
            nc.sync.dma_start(out=first[:], in_=rows[:, i, :])
            return first[:]

        def load_rows(g, rows, label):
            whole = rows_in.tile([P, GROUP, E], BF16, name=label + "_sb")
            nc.sync.dma_start(out=whole[:], in_=rows[:, g * GROUP : (g + 1) * GROUP, :])
            return [whole[:, i, :] for i in range(GROUP)]

        def load_group(g):
            tiles = slice(g * GROUP, (g + 1) * GROUP)
            if g == 0:
                sx_sb, x_sb = [], []
                for half in range(2):
                    for i in (2 * half, 2 * half + 1):
                        sx_sb.append(load_first(sx_rows, "sx", i))
                    for i in (2 * half, 2 * half + 1):
                        x_sb.append(load_first(x_rows, "x", i))
            else:
                sx_sb = load_rows(g, sx_rows, "sx")
                x_sb = load_rows(g, x_rows, "x")
            loaded[g] = {"x": x_sb, "sx": sx_sb}
            load_state(g, "sp", sp_rows)
            load_state(g, "sa", sa_rows)
            load_state(g, "sb", sb_rows)

        def load_state(g, which, rows):
            state_sb = states_in.tile([P, GROUP, D], BF16, name=which + "_sb")
            nc.sync.dma_start(out=state_sb[:], in_=rows[:, g * GROUP : (g + 1) * GROUP, :])
            loaded[g][which] = state_sb

        def load_head():
            sx_sb, x_sb = [], []
            for half in range(2):
                for i in (2 * half, 2 * half + 1):
                    sx_sb.append(load_first(sx_rows, "sx", i))
                for i in (2 * half, 2 * half + 1):
                    x_sb.append(load_first(x_rows, "x", i))
            loaded[0] = {"x": x_sb, "sx": sx_sb}
            loaded[1] = {"sx": load_rows(1, sx_rows, "sx")}
            head_k = load_weight(W_key_words, W_key_scales, "k")
            load_state(0, "sp", sp_rows)
            loaded[1]["x"] = load_rows(1, x_rows, "x")
            head_v = load_weight(W_value_words, W_value_scales, "v")
            load_state(0, "sa", sa_rows)
            load_state(0, "sb", sb_rows)
            load_state(1, "sp", sp_rows)
            load_state(1, "sa", sa_rows)
            load_state(1, "sb", sb_rows)
            return head_k, head_v

        ident = const.tile([P, P], BF16, name="ident")
        make_identity(nc, ident[:])
        ident_f = const.tile([P, P], F32, name="ident_f")
        make_identity(nc, ident_f[:])

        def load_mix(time_mix, label):
            raw = const.tile([P, PACK], BF16, name="mix_raw_" + label)
            nc.scalar.dma_start(out=raw[:], in_=time_mix.rearrange("o (p j) -> (o p) j", j=PACK))
            mix = const.tile([P, PACK], F32, name="mix_" + label)
            nc.vector.tensor_copy(out=mix[:], in_=raw[:])
            rest = const.tile([P, PACK], F32, name="rest_" + label)
            nc.vector.tensor_scalar(
                out=rest[:], in0=raw[:], scalar1=-1.0, scalar2=1.0, op0=ALU.mult, op1=ALU.add
            )
            return mix, rest

        def load_weight(words, scales, label):
            codes = const.tile([P, D * PACK], U8, name="w_codes_" + label, align_bytes=64)
            nc.sync.dma_start(
                out=codes[:].bitcast(I32),
                in_=words[0].rearrange("p n t -> p (n t)").bitcast(I32),
            )
            plane = const.tile([P, D], U8, name="w_plane_" + label, align_bytes=64)
            nc.vector.memset(plane[:].bitcast(I32), 0)
            for q in range(P // QUADRANT):
                nc.sync.dma_start(
                    out=plane[q * QUADRANT : q * QUADRANT + PACK, :].bitcast(I32),
                    in_=scales[0, q * PACK : (q + 1) * PACK, :].bitcast(I32),
                )
            return codes, plane

        mix_k, rest_k = load_mix(time_mix_k, "k")
        mix_v, rest_v = load_mix(time_mix_v, "v")
        weight_k, weight_v = load_head()
        streams = [("k", mix_k, rest_k, weight_k), ("v", mix_v, rest_v, weight_v)]

        halves = D // P
        tf_col = const.tile([P, halves, 2], BF16, name="tf_col")
        nc.scalar.dma_start(out=tf_col[:, :, 0:1], in_=time_first.rearrange("(h p o) -> p h o", p=P, o=1))
        td_col = const.tile([P, halves, 2], BF16, name="td_col")
        nc.scalar.dma_start(out=td_col[:, :, 0:1], in_=time_decay.rearrange("(h p o) -> p h o", p=P, o=1))
        decay = const.tile([P, halves], F32, name="decay")
        nc.scalar.activation(out=decay[:], in_=td_col[:, :, 0], func=FUNC.Exp)
        shift_col = const.tile([P, 2, halves], F32, name="shift_col")
        nc.vector.tensor_scalar_mul(out=shift_col[:, 0, :], in0=tf_col[:, :, 0], scalar1=-1.0)
        nc.vector.tensor_scalar_mul(out=shift_col[:, 1, :], in0=decay[:], scalar1=-1.0)
        shift = psum_c.tile([P, 2, D], F32, name="shift")
        for w in range(2):
            for h in range(halves):
                nc.tensor.transpose(
                    out=shift[:, w, h * P : (h + 1) * P],
                    in_=shift_col[:, w, h : h + 1].to_broadcast([P, P]),
                    identity=ident_f[:],
                )

        shift_sb = const.tile([P, 2, D - MAIN], F32, name="shift_sb")
        nc.scalar.copy(out=shift_sb[:], in_=shift[:, :, MAIN:D])

        def transpose_group(g, which):
            banks = [
                psum_t.tile([P, 2, GROUP_ROWS], BF16, name="%s_t%d" % (which, first_plane))
                for first_plane in range(0, PACK, 2)
            ]
            order = [(i, j) for j in range(PACK) for i in range(GROUP)]
            for i, j in order:
                nc.tensor.transpose(
                    out=banks[j // 2][:, j % 2, i * P : (i + 1) * P],
                    in_=loaded[g][which][i][:, j:E:PACK],
                    identity=ident[:],
                )
            planes = [banks[j // 2][:, j % 2, :] for j in range(PACK)]
            planes_of[(which, g)] = [(slice(0, GROUP_ROWS), planes)]

        def transpose_first_group():
            half_rows = GROUP_ROWS // 2
            planes_of[("sx", 0)] = []
            planes_of[("x", 0)] = []
            for half in range(2):
                for which in ("sx", "x"):
                    bank = psum_t.tile([P, PACK, half_rows], BF16, name="%s_t%d" % (which, 2 * half))
                    for i in range(2):
                        for j in range(PACK):
                            nc.tensor.transpose(
                                out=bank[:, j, i * P : (i + 1) * P],
                                in_=loaded[0][which][2 * half + i][:, j:E:PACK],
                                identity=ident[:],
                            )
                    planes_of[(which, 0)].append(
                        (slice(half * half_rows, (half + 1) * half_rows), [bank[:, j, :] for j in range(PACK)])
                    )

        def transpose_prev(g):
            if g == 0:
                transpose_first_group()
            else:
                transpose_group(g, "sx")

        def transpose_cur(g):
            if g > 0:
                transpose_group(g, "x")

        def scale_prev(m):
            label, mix, rest, weight = streams[m % 2]
            prev_part[m] = stage.tile([P, PACK, GROUP_ROWS], F32, name="prev_part_" + label)
            for rows, planes in planes_of[("sx", m // 2)]:
                for j in range(PACK):
                    nc.scalar.activation(
                        out=prev_part[m][:, j, rows],
                        in_=planes[j],
                        func=FUNC.Copy,
                        scale=rest[:, j : j + 1],
                    )

        def mix_step(m):
            label, mix, rest, weight = streams[m % 2]
            mixed[m] = stage.tile([P, PACK, GROUP_ROWS], BF16, name="mixed_" + label)
            for rows, planes in planes_of[("x", m // 2)]:
                for j in range(PACK):
                    nc.vector.scalar_tensor_tensor(
                        out=mixed[m][:, j, rows],
                        in0=planes[j],
                        scalar=mix[:, j : j + 1],
                        in1=prev_part[m][:, j, rows],
                        op0=ALU.mult,
                        op1=ALU.add,
                    )

        def regroup(m):
            label = streams[m % 2][0]
            grouped[m] = stage.tile([P, GROUP_ROWS, PACK], BF16, name="grouped_" + label, align_bytes=64)
            out_view = grouped[m][:].rearrange("p (c i) j -> p c j i", i=4)
            in_view = mixed[m][:].rearrange("p j (c i) -> p c j i", i=4)
            if m == 0:
                nc.vector.tensor_copy(out=out_view, in_=in_view)
            elif m == 1:
                nc.gpsimd.tensor_scalar(
                    out=out_view, in0=in_view, scalar1=1.0, scalar2=0.0, op0=ALU.mult, op1=ALU.add
                )
            else:
                nc.scalar.copy(out=out_view, in_=in_view)

        def quantise(m):
            label = streams[m % 2][0]
            codes = operands.tile([P, GROUP_ROWS], U32, name="codes_" + label, align_bytes=64)
            plane = operands.tile([P, GROUP_ROWS], U8, name="plane_" + label, align_bytes=64)
            nc.vector.quantize_mx(
                out=codes[:].bitcast(FP8X4),
                scales=plane[:],
                in_=grouped[m][:].rearrange("p r j -> p (r j)"),
            )
            operand[m] = (codes, plane)

        def project(q, stream):
            label, mix, rest, weight = streams[stream]
            codes, plane = operand[2 * (q // 2) + stream]
            w_codes, w_plane = weight
            acc[(label, q)] = (psum_k, psum_v)[stream].tile([P, PAIR, D], F32, name="acc_" + label)
            for i in range(PAIR):
                first_col = ((q % 2) * PAIR + i) * P
                cols = slice(first_col, first_col + P)
                nc.tensor.matmul_mx(
                    out=acc[(label, q)][:, i, :],
                    lhsT=codes[:, cols].bitcast(FP8X4),
                    lhsT_scale=plane[:, cols],
                    rhs=w_codes[:].bitcast(FP8X4),
                    rhs_scale=w_plane[:],
                    start=True,
                    stop=True,
                )

        def project_k(q):
            project(q, 0)

        def project_v(q):
            project(q, 1)

        both = [P, 2, PAIR, D]
        flat = [P, 2, PAIR * D]
        four = [P, 2, 2, PAIR, D]

        def state_of(q, which):
            first_tile = (q % 2) * PAIR
            return loaded[q // 2][which][:, first_tile : first_tile + PAIR, :]

        def states_to_psum(q):
            states_ps[q] = psum_t.tile([P, 2, PAIR, D], BF16, name="sx_t%d" % (2 * (q - DRAIN)))
            for part, which in ((TOP, "sa"), (BOTTOM, "sb")):
                nc.tensor.matmul(
                    out=states_ps[q][:, part].rearrange("p i d -> p (i d)"),
                    lhsT=ident[:],
                    rhs=state_of(q, which).rearrange("p i d -> p (i d)"),
                    start=True,
                    stop=True,
                )

        def state_factor(q, part):
            if q >= DRAIN:
                return states_ps[q][:, part]
            return state_of(q, ("sa", "sb")[part])

        def out_tiles(q):
            return slice(q * PAIR, (q + 1) * PAIR)

        def twice(ap):
            return ap.rearrange("p i d -> p (i d)").unsqueeze(1).to_broadcast(flat)

        def flat_view(tile_ap):
            return tile_ap.rearrange("p w i d -> p w (i d)")

        def gap_of(q):
            gap[q] = work.tile([P, PAIR, D], F32, name="gap")
            nc.vector.tensor_tensor(
                out=gap[q][:], in0=state_of(q, "sp"), in1=acc[("k", q)][:], op=ALU.subtract
            )

        def lead_of(q):
            lead[q] = work.tile(both, F32, name="lead")
            main = D if q == PAIRS - 1 else MAIN
            nc.vector.tensor_tensor(
                out=lead[q][:, :, :, 0:main],
                in0=gap[q][:, :, 0:main].unsqueeze(1).to_broadcast([P, 2, PAIR, main]),
                in1=shift[:, :, 0:main].unsqueeze(2).to_broadcast([P, 2, PAIR, main]),
                op=ALU.add,
            )
            if main == D:
                return
            nc.gpsimd.tensor_tensor(
                out=lead[q][:, :, :, MAIN:D],
                in0=gap[q][:, :, MAIN:D].unsqueeze(1).to_broadcast([P, 2, PAIR, D - MAIN]),
                in1=shift_sb[:].unsqueeze(2).to_broadcast([P, 2, PAIR, D - MAIN]),
                op=ALU.add,
            )

        def new_exponent(q):
            new_p = results.tile([P, PAIR, D], F32, name="new_p")
            nc.vector.scalar_tensor_tensor(
                out=new_p[:].rearrange("p i d -> p (i d)"),
                in0=lead[q][:, 1, :, :].rearrange("p i d -> p (i d)"),
                scalar=0.0,
                in1=acc[("k", q)][:].rearrange("p i d -> p (i d)"),
                op0=ALU.max,
                op1=ALU.add,
            )
            nc.sync.dma_start(out=new_p_rows[:, out_tiles(q), :], in_=new_p[:])

        def weights(q):
            excess = work.tile(both, F32, name="excess")
            nc.scalar.activation(out=excess[:], in_=lead[q][:], func=FUNC.Relu)
            news[q] = work.tile(four, F32, name="news")
            nc.scalar.activation(out=news[q][:, BOTTOM], in_=excess[:], func=FUNC.Exp, scale=-1.0)
            old_w[q] = work.tile(both, F32, name="old_w")
            nc.scalar.activation(out=old_w[q][:], in_=lead[q][:], func=FUNC.Exp)

        def new_term(q):
            nc.vector.tensor_tensor(
                out=flat_view(news[q][:, TOP]), in0=flat_view(news[q][:, BOTTOM]),
                in1=twice(acc[("v", q)][:]), op=ALU.mult,
            )

        def old_b_term(q):
            olds[q] = work.tile(four, F32, name="olds")
            nc.vector.scalar_tensor_tensor(
                out=flat_view(olds[q][:, BOTTOM]), in0=flat_view(old_w[q][:]), scalar=1.0,
                in1=twice(state_factor(q, BOTTOM)), op0=ALU.min, op1=ALU.mult,
            )

        def old_a_term(q):
            nc.vector.scalar_tensor_tensor(
                out=flat_view(olds[q][:, TOP]), in0=flat_view(old_w[q][:]), scalar=1.0,
                in1=twice(state_factor(q, TOP)), op0=ALU.min, op1=ALU.mult,
            )

        stores = {
            (TOP, 0): a_rows, (TOP, 1): new_a_rows, (BOTTOM, 0): b_rows, (BOTTOM, 1): new_b_rows,
        }

        def sums(q):
            if q == PAIRS - 1:
                for part in (BOTTOM, TOP):
                    for w in range(2):
                        last = const.tile([P, PAIR, D], F32, name="last_total_%d_%d" % (part, w))
                        nc.vector.tensor_tensor(
                            out=last[:], in0=olds[q][:, part, w], in1=news[q][:, part, w], op=ALU.add
                        )
                        nc.sync.dma_start(out=stores[(part, w)][:, out_tiles(q), :], in_=last[:])
                return
            total = results.tile(four, F32, name="total")
            if q == PAIRS - 2:
                for part in (BOTTOM, TOP):
                    nc.gpsimd.tensor_tensor(
                        out=total[:, part], in0=olds[q][:, part], in1=news[q][:, part], op=ALU.add
                    )
                    for w in range(2):
                        nc.sync.dma_start(out=stores[(part, w)][:, out_tiles(q), :], in_=total[:, part, w])
                return
            nc.gpsimd.tensor_tensor(out=total[:], in0=olds[q][:], in1=news[q][:], op=ALU.add)
            for part in (TOP, BOTTOM):
                for w in range(2):
                    nc.sync.dma_start(out=stores[(part, w)][:, out_tiles(q), :], in_=total[:, part, w])

        def run(stage_of, index, count):
            if 0 <= index < count:
                stage_of(index)

        def slot(s):
            run(new_term, s, PAIRS)
            run(regroup, s + 2, STEPS)
            run(lead_of, s + 1, PAIRS)
            run(old_b_term, s, PAIRS)
            run(old_a_term, s, PAIRS)
            run(sums, s, PAIRS)
            run(quantise, s + 2, STEPS)
            run(project_k, s + 2, PAIRS)
            run(project_v, s + 1, PAIRS)
            run(scale_prev, s + 3, STEPS)
            if s + 1 >= DRAIN:
                run(states_to_psum, s + 1, PAIRS)
            run(weights, s + 1, PAIRS)
            run(new_exponent, s + 1, PAIRS)
            if s < 0:
                run(gap_of, s + 2, PAIRS)
                run(mix_step, s + 3, STEPS)
            else:
                run(mix_step, s + 3, STEPS)
                run(gap_of, s + 2, PAIRS)
            if s % 2 == 0:
                run(transpose_prev, (s + 4) // 2, GROUPS)
                run(transpose_cur, (s + 4) // 2, GROUPS)
                if (s + 6) // 2 >= 2:
                    run(load_group, (s + 6) // 2, GROUPS)

        for s in range(FIRST_SLOT, 0):
            slot(s)
        with tc.manual_schedule():
            for s in range(PAIRS):
                slot(s)
